import numpy as np
import ml_dtypes


BF16 = ml_dtypes.bfloat16


def bf(x):
    return np.asarray(x, np.float32).astype(BF16)


def f64(x):
    return np.asarray(x).astype(np.float64)


E2M1 = np.array([0.0, 0.5, 1.0, 1.5, 2.0, 3.0, 4.0, 6.0, -0.0, -0.5, -1.0, -1.5, -2.0, -3.0, -4.0, -6.0])


def pack_weight(w, fmt):
    k, n = w.shape
    w = f64(bf(w)).reshape(k // 32, 32, n)
    amax = np.abs(w).max(1)
    if fmt == "e4m3":
        byte = np.frexp(amax)[1] - 1 + 127 - 7
    else:
        mant, ex = np.frexp(amax / 6.0)
        byte = np.where(mant > 0.5, ex, ex - 1) + 127
    byte = np.clip(np.where(amax > 0, byte, 1), 1, 254)
    scaled = (w * np.exp2(127.0 - byte)[:, None, :]).reshape(k, n).astype(np.float32)
    by_word = np.ascontiguousarray(scaled.reshape(k // 512, 128, 4, n).transpose(0, 1, 3, 2))
    if fmt == "e4m3":
        words = by_word.astype(ml_dtypes.float8_e4m3fn).view(np.uint8)
    else:
        c = by_word.astype(ml_dtypes.float4_e2m1fn).view(np.uint8) & 0xF
        words = c[..., 0::2] | (c[..., 1::2] << 4)
    return np.ascontiguousarray(words), np.ascontiguousarray(byte.astype(np.uint8).reshape(k // 512, 16, n))


def unpack_weight(words, scales, fmt):
    g, p, n, _ = words.shape
    if fmt == "e4m3":
        vals = np.ascontiguousarray(words).view(ml_dtypes.float8_e4m3fn).astype(np.float64)
    else:
        nib = np.empty((g, p, n, 4), np.uint8)
        nib[..., 0::2] = words & 0xF
        nib[..., 1::2] = words >> 4
        vals = E2M1[nib]
    vals = vals * np.repeat(np.exp2(scales.astype(np.float64) - 127.0), 8, axis=1)[..., None]
    return vals.transpose(0, 1, 3, 2).reshape(g * 512, n)

def pack4(w):
    words, scales = pack_weight(w, "e2m1")
    return words.reshape(words.shape[0], 128, -1), scales


def unpack4(words, scales):
    return unpack_weight(words.reshape(words.shape[0], 128, -1, 2), scales, "e2m1")


def kspread(k):
    return np.exp2(np.repeat(np.random.randint(-6, 7, k // 32), 32).astype(np.float64))


B, D_IN, D_H, W_RANK, U_RANK = 512, 2048, 4096, 1024, 1024


def sigmoid(v):
    return 1.0 / (1.0 + np.exp(-v))


def setup_inputs():
    s, t = kspread(W_RANK), kspread(U_RANK)
    wx_r = np.random.standard_normal((B, W_RANK)) * s
    uh_r = np.random.standard_normal((B, U_RANK)) * t
    state = bf(np.random.standard_normal((B, D_H)))
    W2 = np.random.standard_normal((D_H, W_RANK)) * 0.7 / np.sqrt(W_RANK) / s
    U2 = np.random.standard_normal((D_H, U_RANK)) * 0.7 / np.sqrt(U_RANK) / t
    wx_r_words, wx_r_scales = pack4(np.ascontiguousarray(wx_r.T))
    uh_r_words, uh_r_scales = pack4(np.ascontiguousarray(uh_r.T))
    W2_words, W2_scales = pack4(np.ascontiguousarray(W2.T))
    U2_words, U2_scales = pack4(np.ascontiguousarray(U2.T))
    return {
        "wx_r_words": wx_r_words,
        "wx_r_scales": wx_r_scales,
        "uh_r_words": uh_r_words,
        "uh_r_scales": uh_r_scales,
        "state": state,
        "W2_words": W2_words,
        "W2_scales": W2_scales,
        "U2_words": U2_words,
        "U2_scales": U2_scales,
        "bias_gate": bf(1.0 + 0.5 * np.random.standard_normal((1, D_H))),
        "bias_update": bf(1.0 + 0.5 * np.random.standard_normal((1, D_H))),
        "zeta": bf(1.0 + 0.1 * np.random.standard_normal((1, 1))),
        "nu": bf(-1.5 + 0.1 * np.random.standard_normal((1, 1))),
    }


def reference(wx_r_words, wx_r_scales, uh_r_words, uh_r_scales, state, W2_words, W2_scales, U2_words, U2_scales, bias_gate, bias_update, zeta, nu):
    wx = unpack4(wx_r_words, wx_r_scales).T @ unpack4(W2_words, W2_scales)
    uh = unpack4(uh_r_words, uh_r_scales).T @ unpack4(U2_words, U2_scales)
    pre = wx + uh
    z = sigmoid(pre + f64(bias_gate))
    h_cand = np.tanh(pre + f64(bias_update))
    return z * f64(state) + (sigmoid(f64(zeta)) * (1.0 - z) + sigmoid(f64(nu))) * h_cand

@@ -1,0 +1,244 @@
+from contextlib import ExitStack
+
+import concourse.mybir as mybir
+from concourse.masks import make_identity
+
+B, D_H, RANK = 512, 4096, 1024
+FLOPS = 2 * B * D_H * 2 * RANK
+
+F32 = mybir.dt.float32
+BF16 = mybir.dt.bfloat16
+U8 = mybir.dt.uint8
+I32 = mybir.dt.int32
+FP4X4 = mybir.dt.float4_e2m1fn_x4
+ACT = mybir.ActivationFunctionType
+ALU = mybir.AluOpType
+
+P = 128
+PASSES = 4
+TOK_TILES = B // P
+N_BLOCKS = D_H // P
+GROUP = 2
+N_GROUPS = N_BLOCKS // GROUP
+
+CODE_CHUNKS = ((0, 512), (512, 1024), (1024, 2048), (2048, 4096))
+SCALE_CHUNKS = ((0, 1024), (1024, 4096))
+
+
+def find_chunk(chunks, channel):
+    for i, (lo, hi) in enumerate(chunks):
+        if lo <= channel < hi:
+            return i, channel - lo
+    raise ValueError("channel outside every chunk")
+
+
+def tile_fastgrnncudacell_pa_kernel(
+    tc,
+    wx_r_words,
+    wx_r_scales,
+    uh_r_words,
+    uh_r_scales,
+    state,
+    W2_words,
+    W2_scales,
+    U2_words,
+    U2_scales,
+    bias_gate,
+    bias_update,
+    zeta,
+    nu,
+    out,
+):
+    nc = tc.nc
+    state_v = state.rearrange("(t p) c -> p t c", p=P)
+    out_v = out.rearrange("(t p) c -> p t c", p=P)
+
+    with ExitStack() as ctx:
+        keep = ctx.enter_context(tc.tile_pool(name="keep", bufs=1))
+        work = ctx.enter_context(tc.tile_pool(name="work", bufs=4))
+        mpsum = ctx.enter_context(tc.psum_pool(name="mpsum", bufs=3))
+        tpsum = ctx.enter_context(tc.psum_pool(name="tpsum", bufs=5))
+        ctx.enter_context(tc.manual_schedule())
+
+        x_codes = keep.tile([P, PASSES, 2 * B], U8, name="x_codes", align_bytes=64)
+        x_scales = keep.tile([P, PASSES, B], U8, name="x_scales", align_bytes=64)
+        w_codes = []
+        st = []
+        for i, (lo, hi) in enumerate(CODE_CHUNKS):
+            w_codes.append(keep.tile([P, PASSES, 2 * (hi - lo)], U8, name="w_codes%d" % i, align_bytes=64))
+            st.append(keep.tile([P, TOK_TILES, hi - lo], BF16, name="st%d" % i))
+        w_scales = []
+        for i, (lo, hi) in enumerate(SCALE_CHUNKS):
+            w_scales.append(keep.tile([P, PASSES, hi - lo], U8, name="w_scales%d" % i, align_bytes=64))
+
+        bias_rows = keep.tile([64, P], BF16, name="bias_rows")
+        bias_sq = keep.tile([P, P], F32, name="bias_sq")
+        bias_t = keep.tile([P, 64], F32, name="bias_t")
+        zeta_b = keep.tile([P, 1], BF16, name="zeta_b")
+        nu_b = keep.tile([P, 1], BF16, name="nu_b")
+        consts = keep.tile([P, 4], F32, name="consts")
+        ident = keep.tile([P, P], F32, name="ident")
+
+        nc.vector.memset(x_scales[:].bitcast(I32), 0)
+        nc.vector.memset(w_scales[0][:].bitcast(I32), 0)
+        nc.vector.memset(bias_sq[:], 0.0)
+        nc.vector.memset(w_scales[1][:].bitcast(I32), 0)
+
+        make_identity(nc, ident[:])
+        nc.gpsimd.dma_start(out=bias_rows[0:32, :], in_=bias_gate.rearrange("o (b c) -> (o b) c", c=P))
+        nc.gpsimd.dma_start(out=bias_rows[32:64, :], in_=bias_update.rearrange("o (b c) -> (o b) c", c=P))
+        nc.gpsimd.dma_start(out=zeta_b[:], in_=zeta.rearrange("a b -> (a b)").partition_broadcast(P))
+        nc.gpsimd.dma_start(out=nu_b[:], in_=nu.rearrange("a b -> (a b)").partition_broadcast(P))
+
+        def load_scales(plane, first_pass, src, lo, hi):
+            for q in range(4):
+                nc.sync.dma_start(
+                    out=plane[32 * q : 32 * q + 4, first_pass : first_pass + 2, :].bitcast(I32),
+                    in_=src[:, 4 * q : 4 * q + 4, lo:hi].rearrange("g r n -> r g n").bitcast(I32),
+                )
+
+        def load_codes(tile, first_pass, src, lo, hi):
+            nc.sync.dma_start(
+                out=tile[:, first_pass : first_pass + 2, :].bitcast(I32),
+                in_=src[:, :, 2 * lo : 2 * hi].rearrange("g p n -> p g n").bitcast(I32),
+            )
+
+        load_codes(x_codes, 0, wx_r_words, 0, B)
+        load_codes(w_codes[0], 0, W2_words, *CODE_CHUNKS[0])
+        load_scales(x_scales, 0, wx_r_scales, 0, B)
+        load_scales(w_scales[0], 0, W2_scales, *SCALE_CHUNKS[0])
+        load_codes(x_codes, 2, uh_r_words, 0, B)
+        load_codes(w_codes[0], 2, U2_words, *CODE_CHUNKS[0])
+        load_scales(x_scales, 2, uh_r_scales, 0, B)
+        load_scales(w_scales[0], 2, U2_scales, *SCALE_CHUNKS[0])
+        nc.sync.dma_start(out=st[0][:], in_=state_v[:, :, CODE_CHUNKS[0][0] : CODE_CHUNKS[0][1]])
+        load_codes(w_codes[1], 0, W2_words, *CODE_CHUNKS[1])
+        load_codes(w_codes[1], 2, U2_words, *CODE_CHUNKS[1])
+        nc.sync.dma_start(out=st[1][:], in_=state_v[:, :, CODE_CHUNKS[1][0] : CODE_CHUNKS[1][1]])
+        load_scales(w_scales[1], 0, W2_scales, *SCALE_CHUNKS[1])
+        load_scales(w_scales[1], 2, U2_scales, *SCALE_CHUNKS[1])
+        for i in (2, 3):
+            load_codes(w_codes[i], 0, W2_words, *CODE_CHUNKS[i])
+            load_codes(w_codes[i], 2, U2_words, *CODE_CHUNKS[i])
+            nc.sync.dma_start(out=st[i][:], in_=state_v[:, :, CODE_CHUNKS[i][0] : CODE_CHUNKS[i][1]])
+
+        nc.scalar.activation(out=consts[:, 0:1], in_=zeta_b[:], func=ACT.Sigmoid)
+        nc.scalar.activation(out=consts[:, 1:2], in_=nu_b[:], func=ACT.Sigmoid)
+        nc.vector.tensor_copy(out=bias_sq[0:64, :], in_=bias_rows[:])
+        nc.vector.tensor_add(out=consts[:, 2:3], in0=consts[:, 0:1], in1=consts[:, 1:2])
+        nc.vector.tensor_scalar_mul(out=consts[:, 3:4], in0=consts[:, 0:1], scalar1=-1.0)
+        a_col = consts[:, 2:3]
+        nsz_col = consts[:, 3:4]
+
+        def turn_biases():
+            bias_ps = tpsum.tile([P, P], F32, name="bias_ps", tag="tr")
+            nc.tensor.transpose(bias_ps[:], bias_sq[:], ident[:])
+            nc.vector.tensor_copy(out=bias_t[:], in_=bias_ps[:, 0:64])
+
+        steps = [[b, b + 1] for b in range(0, N_BLOCKS - 2, 2)] + [[N_BLOCKS - 2], [N_BLOCKS - 1]]
+
+        def on_gpsimd(b):
+            return b % 2 == 0 and b < N_BLOCKS - 2
+
+        pre = {}
+        z_t = {}
+        c_t = {}
+        h_t = {}
+        banks = {}
+
+        def multiply(b, passes):
+            ci, coff = find_chunk(CODE_CHUNKS, P * b)
+            si, soff = find_chunk(SCALE_CHUNKS, P * b)
+            if b not in pre:
+                acc = mpsum.tile([P, B], F32, name="pre", tag="pre")
+                pre[b] = acc
+            for g in passes:
+                nc.tensor.matmul_mx(
+                    out=pre[b][:],
+                    lhsT=w_codes[ci][:, g, 2 * coff : 2 * (coff + P)].bitcast(FP4X4),
+                    lhsT_scale=w_scales[si][:, g, soff : soff + P],
+                    rhs=x_codes[:, g, :].bitcast(FP4X4),
+                    rhs_scale=x_scales[:, g, :],
+                    start=(g == 0),
+                    stop=(g == PASSES - 1),
+                )
+
+        def activate(b):
+            zt = work.tile([P, B], F32, name="z_t", tag="z_t", bufs=6)
+            ct = work.tile([P, B], F32, name="c_t", tag="c_t", bufs=6)
+            nc.scalar.activation(out=zt[:], in_=pre[b][:], func=ACT.Sigmoid, bias=bias_t[:, b : b + 1], scale=1.0)
+            nc.scalar.activation(out=ct[:], in_=pre[b][:], func=ACT.Tanh, bias=bias_t[:, 32 + b : 33 + b], scale=1.0)
+            z_t[b] = zt
+            c_t[b] = ct
+
+        def candidate_weight(b):
+            gt = work.tile([P, B], F32, name="g_t", tag="g_t")
+            ht = work.tile([P, B], F32, name="h_t", tag="h_t")
+            nc.gpsimd.tensor_scalar(out=gt[:], in0=z_t[b][:], scalar1=nsz_col, scalar2=a_col, op0=ALU.mult, op1=ALU.add)
+            nc.gpsimd.tensor_tensor(out=ht[:], in0=gt[:], in1=c_t[b][:], op=ALU.mult)
+            h_t[b] = ht
+
+        def turn(key, src):
+            bank = tpsum.tile([P, TOK_TILES, P], F32, name="tr", tag="tr")
+            for t in range(TOK_TILES):
+                nc.tensor.transpose(bank[:, t, :], src[:, P * t : P * (t + 1)], ident[:])
+            banks[key] = bank
+
+        def state_view(b):
+            ci, coff = find_chunk(CODE_CHUNKS, P * b)
+            return st[ci][:, :, coff : coff + P]
+
+        def finish_pair(ba, bb, o_tile):
+            turn("c", c_t[bb])
+            turn("za", z_t[ba])
+            turn("zb", z_t[bb])
+            turn("h", h_t[ba])
+            u = work.tile([P, TOK_TILES, P], F32, name="u", tag="u")
+            v = work.tile([P, TOK_TILES, P], F32, name="v", tag="v")
+            zs = work.tile([P, TOK_TILES, P], F32, name="zs", tag="zs")
+            nc.vector.scalar_tensor_tensor(out=u[:], in0=banks["c"][:], scalar=nsz_col, in1=state_view(bb), op0=ALU.mult, op1=ALU.add)
+            nc.vector.tensor_tensor(out=zs[:], in0=banks["za"][:], in1=state_view(ba), op=ALU.mult)
+            nc.vector.tensor_tensor(out=v[:], in0=u[:], in1=banks["zb"][:], op=ALU.mult)
+            nc.vector.tensor_tensor(out=o_tile[:, :, 0:P], in0=banks["h"][:], in1=zs[:], op=ALU.add)
+            nc.vector.scalar_tensor_tensor(out=o_tile[:, :, P : 2 * P], in0=banks["c"][:], scalar=a_col, in1=v[:], op0=ALU.mult, op1=ALU.add)
+
+        def finish_single(b, o_tile):
+            turn("c", c_t[b])
+            turn("zb", z_t[b])
+            u = work.tile([P, TOK_TILES, P], F32, name="u", tag="u")
+            v = work.tile([P, TOK_TILES, P], F32, name="v", tag="v")
+            halves = (slice(0, 2), slice(2, 4))
+            for h in halves:
+                nc.vector.scalar_tensor_tensor(out=u[:, h, :], in0=banks["c"][:, h, :], scalar=nsz_col, in1=state_view(b)[:, h, :], op0=ALU.mult, op1=ALU.add)
+            for h in halves:
+                nc.vector.tensor_tensor(out=v[:, h, :], in0=u[:, h, :], in1=banks["zb"][:, h, :], op=ALU.mult)
+            for h in halves:
+                nc.vector.scalar_tensor_tensor(out=o_tile[:, h, :], in0=banks["c"][:, h, :], scalar=a_col, in1=v[:, h, :], op0=ALU.mult, op1=ALU.add)
+
+        for s in range(len(steps) + 1):
+            if s == 0:
+                for b in (0, 1, 2):
+                    multiply(b, (0, 1))
+                turn_biases()
+                for b in (0, 1):
+                    multiply(b, (2, 3))
+            elif s == 1:
+                multiply(2, (2, 3))
+                multiply(3, range(PASSES))
+            elif s < len(steps):
+                for b in steps[s]:
+                    multiply(b, range(PASSES))
+            if s < len(steps):
+                for b in steps[s]:
+                    activate(b)
+                for b in steps[s]:
+                    if on_gpsimd(b):
+                        candidate_weight(b)
+            if s >= 1:
+                blocks = steps[s - 1]
+                o_tile = work.tile([P, TOK_TILES, len(blocks) * P], F32, name="o_tile", tag="o_tile", bufs=6)
+                if len(blocks) == 2:
+                    finish_pair(blocks[0], blocks[1], o_tile)
+                else:
+                    finish_single(blocks[0], o_tile)
+                nc.sync.dma_start(out=out_v[:, :, P * blocks[0] : P * (blocks[-1] + 1)], in_=o_tile[:])

@@ -18,11 +18,19 @@ P = 128
 PASSES = 4
 TOK_TILES = B // P
 N_BLOCKS = D_H // P
-GROUP = 2
-N_GROUPS = N_BLOCKS // GROUP
+N_BANKS = 8
+N_WARM = 8
 
-CODE_CHUNKS = ((0, 512), (512, 1024), (1024, 2048), (2048, 4096))
+A_CH = 1024
+A_HALF = 512
+FIRST_B = A_CH // P
+
+CHUNKS = ((0, 1024), (1024, 2048), (2048, 3072), (3072, 4096))
 SCALE_CHUNKS = ((0, 1024), (1024, 4096))
+
+GPSIMD_BLOCKS = (26, 28, 30)
+GATES_A_AT = (0, 2, 4, 7)
+STORE_A_AT = (2, 5, 7, 10)
 
 
 def find_chunk(chunks, channel):
@@ -56,39 +64,55 @@ def tile_fastgrnncudacell_pa_kernel(
     with ExitStack() as ctx:
         keep = ctx.enter_context(tc.tile_pool(name="keep", bufs=1))
         work = ctx.enter_context(tc.tile_pool(name="work", bufs=4))
-        mpsum = ctx.enter_context(tc.psum_pool(name="mpsum", bufs=3))
-        tpsum = ctx.enter_context(tc.psum_pool(name="tpsum", bufs=5))
+        psum = ctx.enter_context(tc.psum_pool(name="psum", bufs=1))
         ctx.enter_context(tc.manual_schedule())
+
+        free_banks = list(range(N_BANKS))
+
+        def take_bank(shape, name):
+            k = free_banks.pop(0)
+            t = psum.tile(shape, F32, name=name, tag="bank%d" % k)
+            return t, k
+
+        def give_bank(k):
+            free_banks.append(k)
 
         x_codes = keep.tile([P, PASSES, 2 * B], U8, name="x_codes", align_bytes=64)
         x_scales = keep.tile([P, PASSES, B], U8, name="x_scales", align_bytes=64)
         w_codes = []
         st = []
-        for i, (lo, hi) in enumerate(CODE_CHUNKS):
+        for i, (lo, hi) in enumerate(CHUNKS):
             w_codes.append(keep.tile([P, PASSES, 2 * (hi - lo)], U8, name="w_codes%d" % i, align_bytes=64))
             st.append(keep.tile([P, TOK_TILES, hi - lo], BF16, name="st%d" % i))
         w_scales = []
         for i, (lo, hi) in enumerate(SCALE_CHUNKS):
             w_scales.append(keep.tile([P, PASSES, hi - lo], U8, name="w_scales%d" % i, align_bytes=64))
 
-        bias_rows = keep.tile([64, P], BF16, name="bias_rows")
-        bias_sq = keep.tile([P, P], F32, name="bias_sq")
-        bias_t = keep.tile([P, 64], F32, name="bias_t")
+        bias_rows = keep.tile([P, 256], BF16, name="bias_rows")
+        bias_sq = keep.tile([P, 256], F32, name="bias_sq")
+        bias_t = keep.tile([P, 2, 32], F32, name="bias_t")
+        bias_bc = [keep.tile([P, A_CH], F32, name="bias_bc%d" % i) for i in range(2)]
         zeta_b = keep.tile([P, 1], BF16, name="zeta_b")
         nu_b = keep.tile([P, 1], BF16, name="nu_b")
         consts = keep.tile([P, 4], F32, name="consts")
         ident = keep.tile([P, P], F32, name="ident")
+        ident_bf = keep.tile([P, P], BF16, name="ident_bf")
+        warm = keep.tile([P, B], BF16, name="warm")
+        a_col = consts[:, 2:3]
+        nsz_col = consts[:, 3:4]
 
+        nc.vector.memset(warm[:], 0.0)
+        nc.vector.memset(bias_rows[:], 0.0)
         nc.vector.memset(x_scales[:].bitcast(I32), 0)
         nc.vector.memset(w_scales[0][:].bitcast(I32), 0)
-        nc.vector.memset(bias_sq[:], 0.0)
         nc.vector.memset(w_scales[1][:].bitcast(I32), 0)
 
+        nc.gpsimd.dma_start(out=bias_rows[0:16, :], in_=bias_gate.rearrange("o (r c) -> (o r) c", c=256))
+        nc.gpsimd.dma_start(out=bias_rows[16:32, :], in_=bias_update.rearrange("o (r c) -> (o r) c", c=256))
         make_identity(nc, ident[:])
-        nc.gpsimd.dma_start(out=bias_rows[0:32, :], in_=bias_gate.rearrange("o (b c) -> (o b) c", c=P))
-        nc.gpsimd.dma_start(out=bias_rows[32:64, :], in_=bias_update.rearrange("o (b c) -> (o b) c", c=P))
         nc.gpsimd.dma_start(out=zeta_b[:], in_=zeta.rearrange("a b -> (a b)").partition_broadcast(P))
         nc.gpsimd.dma_start(out=nu_b[:], in_=nu.rearrange("a b -> (a b)").partition_broadcast(P))
+        nc.vector.tensor_copy(out=ident_bf[:], in_=ident[:])
 
         def load_scales(plane, first_pass, src, lo, hi):
             for q in range(4):
@@ -103,42 +127,113 @@ def tile_fastgrnncudacell_pa_kernel(
                 in_=src[:, :, 2 * lo : 2 * hi].rearrange("g p n -> p g n").bitcast(I32),
             )
 
+        def load_state(i):
+            nc.sync.dma_start(out=st[i][:], in_=state_v[:, :, CHUNKS[i][0] : CHUNKS[i][1]])
+
         load_codes(x_codes, 0, wx_r_words, 0, B)
-        load_codes(w_codes[0], 0, W2_words, *CODE_CHUNKS[0])
+        load_codes(w_codes[0], 0, W2_words, *CHUNKS[0])
         load_scales(x_scales, 0, wx_r_scales, 0, B)
         load_scales(w_scales[0], 0, W2_scales, *SCALE_CHUNKS[0])
         load_codes(x_codes, 2, uh_r_words, 0, B)
-        load_codes(w_codes[0], 2, U2_words, *CODE_CHUNKS[0])
+        load_codes(w_codes[0], 2, U2_words, *CHUNKS[0])
         load_scales(x_scales, 2, uh_r_scales, 0, B)
         load_scales(w_scales[0], 2, U2_scales, *SCALE_CHUNKS[0])
-        nc.sync.dma_start(out=st[0][:], in_=state_v[:, :, CODE_CHUNKS[0][0] : CODE_CHUNKS[0][1]])
-        load_codes(w_codes[1], 0, W2_words, *CODE_CHUNKS[1])
-        load_codes(w_codes[1], 2, U2_words, *CODE_CHUNKS[1])
-        nc.sync.dma_start(out=st[1][:], in_=state_v[:, :, CODE_CHUNKS[1][0] : CODE_CHUNKS[1][1]])
         load_scales(w_scales[1], 0, W2_scales, *SCALE_CHUNKS[1])
         load_scales(w_scales[1], 2, U2_scales, *SCALE_CHUNKS[1])
+        load_codes(w_codes[1], 0, W2_words, *CHUNKS[1])
+        load_codes(w_codes[1], 2, U2_words, *CHUNKS[1])
+        load_state(0)
+        load_state(1)
         for i in (2, 3):
-            load_codes(w_codes[i], 0, W2_words, *CODE_CHUNKS[i])
-            load_codes(w_codes[i], 2, U2_words, *CODE_CHUNKS[i])
-            nc.sync.dma_start(out=st[i][:], in_=state_v[:, :, CODE_CHUNKS[i][0] : CODE_CHUNKS[i][1]])
+            load_codes(w_codes[i], 0, W2_words, *CHUNKS[i])
+            load_codes(w_codes[i], 2, U2_words, *CHUNKS[i])
+            load_state(i)
 
-        nc.scalar.activation(out=consts[:, 0:1], in_=zeta_b[:], func=ACT.Sigmoid)
-        nc.scalar.activation(out=consts[:, 1:2], in_=nu_b[:], func=ACT.Sigmoid)
-        nc.vector.tensor_copy(out=bias_sq[0:64, :], in_=bias_rows[:])
-        nc.vector.tensor_add(out=consts[:, 2:3], in0=consts[:, 0:1], in1=consts[:, 1:2])
-        nc.vector.tensor_scalar_mul(out=consts[:, 3:4], in0=consts[:, 0:1], scalar1=-1.0)
-        a_col = consts[:, 2:3]
-        nsz_col = consts[:, 3:4]
+        acc_a = {}
+        s1 = {}
+        s2 = {}
+        g_a = {}
+
+        def multiply_a(p, half, passes):
+            if (p, half) not in acc_a:
+                acc_a[(p, half)] = take_bank([P, A_HALF], "acc_a")
+            acc = acc_a[(p, half)][0]
+            for g in passes:
+                nc.tensor.matmul_mx(
+                    out=acc[:],
+                    lhsT=x_codes[:, g, 2 * P * p : 2 * P * (p + 1)].bitcast(FP4X4),
+                    lhsT_scale=x_scales[:, g, P * p : P * (p + 1)],
+                    rhs=w_codes[0][:, g, 2 * A_HALF * half : 2 * A_HALF * (half + 1)].bitcast(FP4X4),
+                    rhs_scale=w_scales[0][:, g, A_HALF * half : A_HALF * (half + 1)],
+                    start=(g == 0),
+                    stop=(g == PASSES - 1),
+                )
+
+        def add_biases(p, half):
+            if p not in s1:
+                s1_tile = work.tile([P, A_CH], F32, name="s1", tag="s1")
+                s2_tile = work.tile([P, A_CH], F32, name="s2", tag="s2")
+                s1[p] = s1_tile
+                s2[p] = s2_tile
+            acc, k = acc_a[(p, half)]
+            cols = slice(A_HALF * half, A_HALF * (half + 1))
+            nc.vector.tensor_tensor(out=s1[p][:, cols], in0=acc[:], in1=bias_bc[0][:, cols], op=ALU.add)
+            nc.vector.tensor_tensor(out=s2[p][:, cols], in0=acc[:], in1=bias_bc[1][:, cols], op=ALU.add)
+            give_bank(k)
+
+        def gates_a(p):
+            g_tile = work.tile([P, A_CH], F32, name="g_a", tag="g_a")
+            g_a[p] = g_tile
+            nc.scalar.activation(out=s1[p][:], in_=s1[p][:], func=ACT.Sigmoid)
+            nc.scalar.activation(out=s2[p][:], in_=s2[p][:], func=ACT.Tanh)
+            nc.scalar.activation(out=g_tile[:], in_=s1[p][:], func=ACT.Identity, bias=a_col, scale=nsz_col)
+            nc.gpsimd.tensor_tensor(out=s1[p][:], in0=s1[p][:], in1=st[0][:, p, :], op=ALU.mult)
+            nc.gpsimd.tensor_tensor(out=g_tile[:], in0=g_tile[:], in1=s2[p][:], op=ALU.mult)
+            nc.gpsimd.tensor_tensor(out=s1[p][:], in0=s1[p][:], in1=g_tile[:], op=ALU.add)
+
+        def store_a(p):
+            nc.sync.dma_start(out=out[P * p : P * (p + 1), 0:A_CH], in_=s1[p][:])
+
+        def warm_up():
+            t, k = take_bank([P, B], "warm_ps")
+            for i in range(N_WARM):
+                nc.tensor.matmul(out=t[:], lhsT=warm[:, 0:P], rhs=warm[:], start=True, stop=True)
+            give_bank(k)
+
+        def spread_biases():
+            for i in range(2):
+                for half in range(A_CH // A_HALF):
+                    t, k = take_bank([P, A_HALF], "bc_ps")
+                    for e in range(2):
+                        r = 16 * i + 2 * half + e
+                        nc.tensor.matmul(
+                            out=t[:, 256 * e : 256 * (e + 1)],
+                            lhsT=ident_bf[:, r : r + 1].to_broadcast([P, P]),
+                            rhs=bias_rows[:],
+                            start=True,
+                            stop=True,
+                        )
+                    nc.scalar.copy(out=bias_bc[i][:, A_HALF * half : A_HALF * (half + 1)], in_=t[:])
+                    give_bank(k)
 
         def turn_biases():
-            bias_ps = tpsum.tile([P, P], F32, name="bias_ps", tag="tr")
-            nc.tensor.transpose(bias_ps[:], bias_sq[:], ident[:])
-            nc.vector.tensor_copy(out=bias_t[:], in_=bias_ps[:, 0:64])
+            nc.vector.tensor_copy(out=bias_sq[:], in_=bias_rows[:])
+            t, k = take_bank([P, 2, P], "bias_ps")
+            for e in range(2):
+                nc.tensor.transpose(t[:, e, :], bias_sq[:, P * e : P * (e + 1)], ident[:])
+            nc.vector.tensor_copy(out=bias_t[:], in_=t[:, :, 0:32])
+            give_bank(k)
 
-        steps = [[b, b + 1] for b in range(0, N_BLOCKS - 2, 2)] + [[N_BLOCKS - 2], [N_BLOCKS - 1]]
+        def make_consts():
+            nc.scalar.activation(out=consts[:, 0:1], in_=zeta_b[:], func=ACT.Sigmoid)
+            nc.scalar.activation(out=consts[:, 1:2], in_=nu_b[:], func=ACT.Sigmoid)
+            nc.vector.tensor_add(out=consts[:, 2:3], in0=consts[:, 0:1], in1=consts[:, 1:2])
+            nc.vector.tensor_scalar_mul(out=consts[:, 3:4], in0=consts[:, 0:1], scalar1=-1.0)
+
+        steps = [[b, b + 1] for b in range(FIRST_B, N_BLOCKS - 2, 2)] + [[N_BLOCKS - 2], [N_BLOCKS - 1]]
 
         def on_gpsimd(b):
-            return b % 2 == 0 and b < N_BLOCKS - 2
+            return b in GPSIMD_BLOCKS
 
         pre = {}
         z_t = {}
@@ -146,15 +241,13 @@ def tile_fastgrnncudacell_pa_kernel(
         h_t = {}
         banks = {}
 
-        def multiply(b, passes):
-            ci, coff = find_chunk(CODE_CHUNKS, P * b)
+        def multiply(b):
+            ci, coff = find_chunk(CHUNKS, P * b)
             si, soff = find_chunk(SCALE_CHUNKS, P * b)
-            if b not in pre:
-                acc = mpsum.tile([P, B], F32, name="pre", tag="pre")
-                pre[b] = acc
-            for g in passes:
+            pre[b] = take_bank([P, B], "pre")
+            for g in range(PASSES):
                 nc.tensor.matmul_mx(
-                    out=pre[b][:],
+                    out=pre[b][0][:],
                     lhsT=w_codes[ci][:, g, 2 * coff : 2 * (coff + P)].bitcast(FP4X4),
                     lhsT_scale=w_scales[si][:, g, soff : soff + P],
                     rhs=x_codes[:, g, :].bitcast(FP4X4),
@@ -166,69 +259,94 @@ def tile_fastgrnncudacell_pa_kernel(
         def activate(b):
             zt = work.tile([P, B], F32, name="z_t", tag="z_t", bufs=6)
             ct = work.tile([P, B], F32, name="c_t", tag="c_t", bufs=6)
-            nc.scalar.activation(out=zt[:], in_=pre[b][:], func=ACT.Sigmoid, bias=bias_t[:, b : b + 1], scale=1.0)
-            nc.scalar.activation(out=ct[:], in_=pre[b][:], func=ACT.Tanh, bias=bias_t[:, 32 + b : 33 + b], scale=1.0)
+            acc, k = pre[b]
+            r, e = b // 2, b % 2
+            nc.scalar.activation(out=zt[:], in_=acc[:], func=ACT.Sigmoid, bias=bias_t[:, e, r : r + 1], scale=1.0)
+            nc.scalar.activation(out=ct[:], in_=acc[:], func=ACT.Tanh, bias=bias_t[:, e, 16 + r : 17 + r], scale=1.0)
+            give_bank(k)
             z_t[b] = zt
             c_t[b] = ct
 
         def candidate_weight(b):
-            gt = work.tile([P, B], F32, name="g_t", tag="g_t")
-            ht = work.tile([P, B], F32, name="h_t", tag="h_t")
+            gt = work.tile([P, B], F32, name="g_t", tag="g_t", bufs=2)
+            ht = work.tile([P, B], F32, name="h_t", tag="h_t", bufs=2)
             nc.gpsimd.tensor_scalar(out=gt[:], in0=z_t[b][:], scalar1=nsz_col, scalar2=a_col, op0=ALU.mult, op1=ALU.add)
             nc.gpsimd.tensor_tensor(out=ht[:], in0=gt[:], in1=c_t[b][:], op=ALU.mult)
             h_t[b] = ht
 
         def turn(key, src):
-            bank = tpsum.tile([P, TOK_TILES, P], F32, name="tr", tag="tr")
+            bank, k = take_bank([P, TOK_TILES, P], "tr")
             for t in range(TOK_TILES):
                 nc.tensor.transpose(bank[:, t, :], src[:, P * t : P * (t + 1)], ident[:])
-            banks[key] = bank
+            banks[key] = (bank, k)
 
         def state_view(b):
-            ci, coff = find_chunk(CODE_CHUNKS, P * b)
+            ci, coff = find_chunk(CHUNKS, P * b)
             return st[ci][:, :, coff : coff + P]
 
-        def finish_pair(ba, bb, o_tile):
-            turn("c", c_t[bb])
-            turn("za", z_t[ba])
-            turn("zb", z_t[bb])
-            turn("h", h_t[ba])
-            u = work.tile([P, TOK_TILES, P], F32, name="u", tag="u")
-            v = work.tile([P, TOK_TILES, P], F32, name="v", tag="v")
-            zs = work.tile([P, TOK_TILES, P], F32, name="zs", tag="zs")
-            nc.vector.scalar_tensor_tensor(out=u[:], in0=banks["c"][:], scalar=nsz_col, in1=state_view(bb), op0=ALU.mult, op1=ALU.add)
-            nc.vector.tensor_tensor(out=zs[:], in0=banks["za"][:], in1=state_view(ba), op=ALU.mult)
-            nc.vector.tensor_tensor(out=v[:], in0=u[:], in1=banks["zb"][:], op=ALU.mult)
-            nc.vector.tensor_tensor(out=o_tile[:, :, 0:P], in0=banks["h"][:], in1=zs[:], op=ALU.add)
-            nc.vector.scalar_tensor_tensor(out=o_tile[:, :, P : 2 * P], in0=banks["c"][:], scalar=a_col, in1=v[:], op0=ALU.mult, op1=ALU.add)
+        def finish(blocks, o_tile):
+            turns = []
+            ops = []
+            halves = (slice(0, 4),) if len(blocks) == 2 else (slice(0, 2), slice(2, 4))
+            for i, b in enumerate(blocks):
+                o_view = o_tile[:, :, P * i : P * (i + 1)]
+                t1 = work.tile([P, TOK_TILES, P], F32, name="t1", tag="t1")
+                if on_gpsimd(b):
+                    turns.append([(z_t[b], (b, "z")), (h_t[b], (b, "h"))])
+                    ops.append([("zs", b, t1, o_view), ("oh", b, t1, o_view)])
+                else:
+                    t2 = work.tile([P, TOK_TILES, P], F32, name="t2", tag="t2")
+                    turns.append([(c_t[b], (b, "c")), (z_t[b], (b, "z"))])
+                    ops.append([("u", b, t1, t2), ("v", b, t1, t2), ("oc", b, t2, o_view)])
+            order = sorted(range(len(blocks)), key=lambda i: -len(ops[i]))
+            for level in range(2):
+                for i in order:
+                    turn(turns[i][level][1], turns[i][level][0])
+            for level in range(3):
+                for i in order:
+                    if level >= len(ops[i]):
+                        continue
+                    kind, b, x, y = ops[i][level]
+                    for h in halves:
+                        if kind == "zs":
+                            nc.vector.tensor_tensor(out=x[:, h, :], in0=banks[(b, "z")][0][:, h, :], in1=state_view(b)[:, h, :], op=ALU.mult)
+                        elif kind == "oh":
+                            nc.vector.tensor_tensor(out=y[:, h, :], in0=banks[(b, "h")][0][:, h, :], in1=x[:, h, :], op=ALU.add)
+                        elif kind == "u":
+                            nc.vector.scalar_tensor_tensor(out=x[:, h, :], in0=banks[(b, "c")][0][:, h, :], scalar=nsz_col, in1=state_view(b)[:, h, :], op0=ALU.mult, op1=ALU.add)
+                        elif kind == "v":
+                            nc.vector.tensor_tensor(out=y[:, h, :], in0=x[:, h, :], in1=banks[(b, "z")][0][:, h, :], op=ALU.mult)
+                        else:
+                            nc.vector.scalar_tensor_tensor(out=y[:, h, :], in0=banks[(b, "c")][0][:, h, :], scalar=a_col, in1=x[:, h, :], op0=ALU.mult, op1=ALU.add)
+                    if kind == "zs" or kind == "v":
+                        give_bank(banks[(b, "z")][1])
+                    elif kind == "oh":
+                        give_bank(banks[(b, "h")][1])
+                    elif kind == "oc":
+                        give_bank(banks[(b, "c")][1])
 
-        def finish_single(b, o_tile):
-            turn("c", c_t[b])
-            turn("zb", z_t[b])
-            u = work.tile([P, TOK_TILES, P], F32, name="u", tag="u")
-            v = work.tile([P, TOK_TILES, P], F32, name="v", tag="v")
-            halves = (slice(0, 2), slice(2, 4))
-            for h in halves:
-                nc.vector.scalar_tensor_tensor(out=u[:, h, :], in0=banks["c"][:, h, :], scalar=nsz_col, in1=state_view(b)[:, h, :], op0=ALU.mult, op1=ALU.add)
-            for h in halves:
-                nc.vector.tensor_tensor(out=v[:, h, :], in0=u[:, h, :], in1=banks["zb"][:, h, :], op=ALU.mult)
-            for h in halves:
-                nc.vector.scalar_tensor_tensor(out=o_tile[:, h, :], in0=banks["c"][:, h, :], scalar=a_col, in1=v[:, h, :], op0=ALU.mult, op1=ALU.add)
+        units = [(p, half) for p in range(TOK_TILES) for half in range(A_CH // A_HALF)]
+        warm_up()
+        for p, half in units[0:4]:
+            multiply_a(p, half, (0, 1))
+        spread_biases()
+        turn_biases()
+        make_consts()
+        for p, half in units[4:8]:
+            multiply_a(p, half, (0, 1))
+        for p, half in units:
+            multiply_a(p, half, (2, 3))
+            add_biases(p, half)
 
         for s in range(len(steps) + 1):
-            if s == 0:
-                for b in (0, 1, 2):
-                    multiply(b, (0, 1))
-                turn_biases()
-                for b in (0, 1):
-                    multiply(b, (2, 3))
-            elif s == 1:
-                multiply(2, (2, 3))
-                multiply(3, range(PASSES))
-            elif s < len(steps):
-                for b in steps[s]:
-                    multiply(b, range(PASSES))
+            for p in range(TOK_TILES):
+                if GATES_A_AT[p] == s:
+                    gates_a(p)
+                if STORE_A_AT[p] == s:
+                    store_a(p)
             if s < len(steps):
+                for b in steps[s]:
+                    multiply(b)
                 for b in steps[s]:
                     activate(b)
                 for b in steps[s]:
@@ -236,9 +354,6 @@ def tile_fastgrnncudacell_pa_kernel(
                         candidate_weight(b)
             if s >= 1:
                 blocks = steps[s - 1]
-                o_tile = work.tile([P, TOK_TILES, len(blocks) * P], F32, name="o_tile", tag="o_tile", bufs=6)
-                if len(blocks) == 2:
-                    finish_pair(blocks[0], blocks[1], o_tile)
-                else:
-                    finish_single(blocks[0], o_tile)
+                o_tile = work.tile([P, TOK_TILES, len(blocks) * P], F32, name="o_tile", tag="o_tile")
+                finish(blocks, o_tile)
                 nc.sync.dma_start(out=out_v[:, :, P * blocks[0] : P * (blocks[-1] + 1)], in_=o_tile[:])

@@ -19,7 +19,7 @@ PASSES = 4
 TOK_TILES = B // P
 N_BLOCKS = D_H // P
 N_BANKS = 8
-N_WARM = 8
+N_WARM = (6, 4)
 
 A_CH = 1024
 A_HALF = 512
@@ -101,18 +101,15 @@ def tile_fastgrnncudacell_pa_kernel(
         a_col = consts[:, 2:3]
         nsz_col = consts[:, 3:4]
 
-        nc.vector.memset(warm[:], 0.0)
-        nc.vector.memset(bias_rows[:], 0.0)
-        nc.vector.memset(x_scales[:].bitcast(I32), 0)
-        nc.vector.memset(w_scales[0][:].bitcast(I32), 0)
-        nc.vector.memset(w_scales[1][:].bitcast(I32), 0)
-
-        nc.gpsimd.dma_start(out=bias_rows[0:16, :], in_=bias_gate.rearrange("o (r c) -> (o r) c", c=256))
-        nc.gpsimd.dma_start(out=bias_rows[16:32, :], in_=bias_update.rearrange("o (r c) -> (o r) c", c=256))
+        nc.gpsimd.memset(bias_rows[:], 0.0)
+        nc.gpsimd.memset(warm[:], 0.0)
         make_identity(nc, ident[:])
         nc.gpsimd.dma_start(out=zeta_b[:], in_=zeta.rearrange("a b -> (a b)").partition_broadcast(P))
         nc.gpsimd.dma_start(out=nu_b[:], in_=nu.rearrange("a b -> (a b)").partition_broadcast(P))
+        nc.vector.memset(x_scales[:].bitcast(I32), 0)
+        nc.vector.memset(w_scales[0][:].bitcast(I32), 0)
         nc.vector.tensor_copy(out=ident_bf[:], in_=ident[:])
+        nc.vector.memset(w_scales[1][:].bitcast(I32), 0)
 
         def load_scales(plane, first_pass, src, lo, hi):
             for q in range(4):
@@ -130,6 +127,8 @@ def tile_fastgrnncudacell_pa_kernel(
         def load_state(i):
             nc.sync.dma_start(out=st[i][:], in_=state_v[:, :, CHUNKS[i][0] : CHUNKS[i][1]])
 
+        nc.sync.dma_start(out=bias_rows[0:16, :], in_=bias_gate.rearrange("o (r c) -> (o r) c", c=256))
+        nc.sync.dma_start(out=bias_rows[16:32, :], in_=bias_update.rearrange("o (r c) -> (o r) c", c=256))
         load_codes(x_codes, 0, wx_r_words, 0, B)
         load_codes(w_codes[0], 0, W2_words, *CHUNKS[0])
         load_scales(x_scales, 0, wx_r_scales, 0, B)
@@ -194,9 +193,9 @@ def tile_fastgrnncudacell_pa_kernel(
         def store_a(p):
             nc.sync.dma_start(out=out[P * p : P * (p + 1), 0:A_CH], in_=s1[p][:])
 
-        def warm_up():
+        def warm_up(n):
             t, k = take_bank([P, B], "warm_ps")
-            for i in range(N_WARM):
+            for i in range(n):
                 nc.tensor.matmul(out=t[:], lhsT=warm[:, 0:P], rhs=warm[:], start=True, stop=True)
             give_bank(k)
 
@@ -326,13 +325,12 @@ def tile_fastgrnncudacell_pa_kernel(
                         give_bank(banks[(b, "c")][1])
 
         units = [(p, half) for p in range(TOK_TILES) for half in range(A_CH // A_HALF)]
-        warm_up()
-        for p, half in units[0:4]:
-            multiply_a(p, half, (0, 1))
+        warm_up(N_WARM[0])
         spread_biases()
         turn_biases()
         make_consts()
-        for p, half in units[4:8]:
+        warm_up(N_WARM[1])
+        for p, half in units:
             multiply_a(p, half, (0, 1))
         for p, half in units:
             multiply_a(p, half, (2, 3))
@@ -356,4 +354,9 @@ def tile_fastgrnncudacell_pa_kernel(
                 blocks = steps[s - 1]
                 o_tile = work.tile([P, TOK_TILES, len(blocks) * P], F32, name="o_tile", tag="o_tile")
                 finish(blocks, o_tile)
-                nc.sync.dma_start(out=out_v[:, :, P * blocks[0] : P * (blocks[-1] + 1)], in_=o_tile[:])
+                cols = slice(P * blocks[0], P * (blocks[-1] + 1))
+                if s == len(steps):
+                    for h in (slice(0, 2), slice(2, 4)):
+                        nc.sync.dma_start(out=out_v[:, h, cols], in_=o_tile[:, h, :])
+                else:
+                    nc.sync.dma_start(out=out_v[:, :, cols], in_=o_tile[:])

@@ -19,7 +19,7 @@ PASSES = 4
 TOK_TILES = B // P
 N_BLOCKS = D_H // P
 N_BANKS = 8
-N_WARM = (6, 4)
+N_WARM = (4, 3)
 
 A_CH = 1024
 A_HALF = 512
@@ -89,6 +89,8 @@ def tile_fastgrnncudacell_pa_kernel(
             w_scales.append(keep.tile([P, PASSES, hi - lo], U8, name="w_scales%d" % i, align_bytes=64))
 
         bias_rows = keep.tile([P, 256], BF16, name="bias_rows")
+        bias_a = keep.tile([P, A_HALF], BF16, name="bias_a")
+        sel = keep.tile([P, 4, P], BF16, name="sel")
         bias_sq = keep.tile([P, 256], F32, name="bias_sq")
         bias_t = keep.tile([P, 2, 32], F32, name="bias_t")
         bias_bc = [keep.tile([P, A_CH], F32, name="bias_bc%d" % i) for i in range(2)]
@@ -96,20 +98,23 @@ def tile_fastgrnncudacell_pa_kernel(
         nu_b = keep.tile([P, 1], BF16, name="nu_b")
         consts = keep.tile([P, 4], F32, name="consts")
         ident = keep.tile([P, P], F32, name="ident")
-        ident_bf = keep.tile([P, P], BF16, name="ident_bf")
         warm = keep.tile([P, B], BF16, name="warm")
         a_col = consts[:, 2:3]
         nsz_col = consts[:, 3:4]
 
-        nc.gpsimd.memset(bias_rows[:], 0.0)
-        nc.gpsimd.memset(warm[:], 0.0)
-        make_identity(nc, ident[:])
-        nc.gpsimd.dma_start(out=zeta_b[:], in_=zeta.rearrange("a b -> (a b)").partition_broadcast(P))
-        nc.gpsimd.dma_start(out=nu_b[:], in_=nu.rearrange("a b -> (a b)").partition_broadcast(P))
+        nc.vector.memset(bias_a[:].bitcast(I32), 0)
         nc.vector.memset(x_scales[:].bitcast(I32), 0)
         nc.vector.memset(w_scales[0][:].bitcast(I32), 0)
-        nc.vector.tensor_copy(out=ident_bf[:], in_=ident[:])
+        nc.vector.memset(warm[:].bitcast(I32), 0)
+        nc.vector.memset(sel[:].bitcast(I32), 0)
+        for j in range(4):
+            nc.vector.memset(sel[32 * j : 32 * j + 1, j, :], 1.0)
+        nc.vector.memset(bias_rows[:].bitcast(I32), 0)
         nc.vector.memset(w_scales[1][:].bitcast(I32), 0)
+
+        make_identity(nc, ident[:])
+        nc.gpsimd.dma_start(out=bias_rows[0:16, :], in_=bias_gate.rearrange("o (r c) -> (o r) c", c=256))
+        nc.gpsimd.dma_start(out=bias_rows[16:32, :], in_=bias_update.rearrange("o (r c) -> (o r) c", c=256))
 
         def load_scales(plane, first_pass, src, lo, hi):
             for q in range(4):
@@ -127,16 +132,18 @@ def tile_fastgrnncudacell_pa_kernel(
         def load_state(i):
             nc.sync.dma_start(out=st[i][:], in_=state_v[:, :, CHUNKS[i][0] : CHUNKS[i][1]])
 
-        nc.sync.dma_start(out=bias_rows[0:16, :], in_=bias_gate.rearrange("o (r c) -> (o r) c", c=256))
-        nc.sync.dma_start(out=bias_rows[16:32, :], in_=bias_update.rearrange("o (r c) -> (o r) c", c=256))
         load_codes(x_codes, 0, wx_r_words, 0, B)
         load_codes(w_codes[0], 0, W2_words, *CHUNKS[0])
+        for i, bias in enumerate((bias_gate, bias_update)):
+            nc.sync.dma_start(out=bias_a[64 * i : 64 * (i + 1) : 32, :], in_=bias.rearrange("o (r c) -> (o r) c", c=A_HALF)[0:2, :])
         load_scales(x_scales, 0, wx_r_scales, 0, B)
         load_scales(w_scales[0], 0, W2_scales, *SCALE_CHUNKS[0])
         load_codes(x_codes, 2, uh_r_words, 0, B)
         load_codes(w_codes[0], 2, U2_words, *CHUNKS[0])
         load_scales(x_scales, 2, uh_r_scales, 0, B)
         load_scales(w_scales[0], 2, U2_scales, *SCALE_CHUNKS[0])
+        nc.sync.dma_start(out=zeta_b[:], in_=zeta.rearrange("a b -> (a b)").partition_broadcast(P))
+        nc.sync.dma_start(out=nu_b[:], in_=nu.rearrange("a b -> (a b)").partition_broadcast(P))
         load_scales(w_scales[1], 0, W2_scales, *SCALE_CHUNKS[1])
         load_scales(w_scales[1], 2, U2_scales, *SCALE_CHUNKS[1])
         load_codes(w_codes[1], 0, W2_words, *CHUNKS[1])
@@ -186,8 +193,8 @@ def tile_fastgrnncudacell_pa_kernel(
             nc.scalar.activation(out=s1[p][:], in_=s1[p][:], func=ACT.Sigmoid)
             nc.scalar.activation(out=s2[p][:], in_=s2[p][:], func=ACT.Tanh)
             nc.scalar.activation(out=g_tile[:], in_=s1[p][:], func=ACT.Identity, bias=a_col, scale=nsz_col)
-            nc.gpsimd.tensor_tensor(out=s1[p][:], in0=s1[p][:], in1=st[0][:, p, :], op=ALU.mult)
             nc.gpsimd.tensor_tensor(out=g_tile[:], in0=g_tile[:], in1=s2[p][:], op=ALU.mult)
+            nc.gpsimd.tensor_tensor(out=s1[p][:], in0=s1[p][:], in1=st[0][:, p, :], op=ALU.mult)
             nc.gpsimd.tensor_tensor(out=s1[p][:], in0=s1[p][:], in1=g_tile[:], op=ALU.add)
 
         def store_a(p):
@@ -203,31 +210,16 @@ def tile_fastgrnncudacell_pa_kernel(
             for i in range(2):
                 for half in range(A_CH // A_HALF):
                     t, k = take_bank([P, A_HALF], "bc_ps")
-                    for e in range(2):
-                        r = 16 * i + 2 * half + e
-                        nc.tensor.matmul(
-                            out=t[:, 256 * e : 256 * (e + 1)],
-                            lhsT=ident_bf[:, r : r + 1].to_broadcast([P, P]),
-                            rhs=bias_rows[:],
-                            start=True,
-                            stop=True,
-                        )
+                    nc.tensor.matmul(out=t[:], lhsT=sel[:, 2 * i + half, :], rhs=bias_a[:], start=True, stop=True)
                     nc.scalar.copy(out=bias_bc[i][:, A_HALF * half : A_HALF * (half + 1)], in_=t[:])
                     give_bank(k)
 
         def turn_biases():
-            nc.vector.tensor_copy(out=bias_sq[:], in_=bias_rows[:])
             t, k = take_bank([P, 2, P], "bias_ps")
             for e in range(2):
                 nc.tensor.transpose(t[:, e, :], bias_sq[:, P * e : P * (e + 1)], ident[:])
-            nc.vector.tensor_copy(out=bias_t[:], in_=t[:, :, 0:32])
+            nc.scalar.copy(out=bias_t[:], in_=t[:, :, 0:32])
             give_bank(k)
-
-        def make_consts():
-            nc.scalar.activation(out=consts[:, 0:1], in_=zeta_b[:], func=ACT.Sigmoid)
-            nc.scalar.activation(out=consts[:, 1:2], in_=nu_b[:], func=ACT.Sigmoid)
-            nc.vector.tensor_add(out=consts[:, 2:3], in0=consts[:, 0:1], in1=consts[:, 1:2])
-            nc.vector.tensor_scalar_mul(out=consts[:, 3:4], in0=consts[:, 0:1], scalar1=-1.0)
 
         steps = [[b, b + 1] for b in range(FIRST_B, N_BLOCKS - 2, 2)] + [[N_BLOCKS - 2], [N_BLOCKS - 1]]
 
@@ -327,18 +319,24 @@ def tile_fastgrnncudacell_pa_kernel(
         units = [(p, half) for p in range(TOK_TILES) for half in range(A_CH // A_HALF)]
         warm_up(N_WARM[0])
         spread_biases()
-        turn_biases()
-        make_consts()
         warm_up(N_WARM[1])
         for p, half in units:
             multiply_a(p, half, (0, 1))
-        for p, half in units:
+        nc.scalar.copy(out=bias_sq[:], in_=bias_rows[:])
+        nc.scalar.activation(out=consts[:, 0:1], in_=zeta_b[:], func=ACT.Sigmoid)
+        nc.scalar.activation(out=consts[:, 1:2], in_=nu_b[:], func=ACT.Sigmoid)
+        for i, (p, half) in enumerate(units):
             multiply_a(p, half, (2, 3))
             add_biases(p, half)
+            if i == 3:
+                nc.vector.tensor_add(out=consts[:, 2:3], in0=consts[:, 0:1], in1=consts[:, 1:2])
+                nc.vector.tensor_scalar_mul(out=consts[:, 3:4], in0=consts[:, 0:1], scalar1=-1.0)
+        gates_a(0)
+        turn_biases()
 
         for s in range(len(steps) + 1):
             for p in range(TOK_TILES):
-                if GATES_A_AT[p] == s:
+                if GATES_A_AT[p] == s and p > 0:
                     gates_a(p)
                 if STORE_A_AT[p] == s:
                     store_a(p)
@@ -354,9 +352,4 @@ def tile_fastgrnncudacell_pa_kernel(
                 blocks = steps[s - 1]
                 o_tile = work.tile([P, TOK_TILES, len(blocks) * P], F32, name="o_tile", tag="o_tile")
                 finish(blocks, o_tile)
-                cols = slice(P * blocks[0], P * (blocks[-1] + 1))
-                if s == len(steps):
-                    for h in (slice(0, 2), slice(2, 4)):
-                        nc.sync.dma_start(out=out_v[:, h, cols], in_=o_tile[:, h, :])
-                else:
-                    nc.sync.dma_start(out=out_v[:, :, cols], in_=o_tile[:])
+                nc.sync.dma_start(out=out_v[:, :, P * blocks[0] : P * (blocks[-1] + 1)], in_=o_tile[:])

@@ -19,14 +19,14 @@ PASSES = 4
 TOK_TILES = B // P
 N_BLOCKS = D_H // P
 N_BANKS = 8
-N_WARM = (4, 3)
+N_WARM = 8
 
 A_CH = 1024
 A_HALF = 512
 FIRST_B = A_CH // P
 
 CHUNKS = ((0, 1024), (1024, 2048), (2048, 3072), (3072, 4096))
-SCALE_CHUNKS = ((0, 1024), (1024, 4096))
+SCALE_CHUNKS = ((0, 1024), (1024, 2048), (2048, 4096))
 
 GPSIMD_BLOCKS = (26, 28, 30)
 GATES_A_AT = (0, 2, 4, 7)
@@ -89,8 +89,6 @@ def tile_fastgrnncudacell_pa_kernel(
             w_scales.append(keep.tile([P, PASSES, hi - lo], U8, name="w_scales%d" % i, align_bytes=64))
 
         bias_rows = keep.tile([P, 256], BF16, name="bias_rows")
-        bias_a = keep.tile([P, A_HALF], BF16, name="bias_a")
-        sel = keep.tile([P, 4, P], BF16, name="sel")
         bias_sq = keep.tile([P, 256], F32, name="bias_sq")
         bias_t = keep.tile([P, 2, 32], F32, name="bias_t")
         bias_bc = [keep.tile([P, A_CH], F32, name="bias_bc%d" % i) for i in range(2)]
@@ -98,23 +96,25 @@ def tile_fastgrnncudacell_pa_kernel(
         nu_b = keep.tile([P, 1], BF16, name="nu_b")
         consts = keep.tile([P, 4], F32, name="consts")
         ident = keep.tile([P, P], F32, name="ident")
+        ident_bf = keep.tile([P, P], BF16, name="ident_bf")
         warm = keep.tile([P, B], BF16, name="warm")
         a_col = consts[:, 2:3]
         nsz_col = consts[:, 3:4]
 
-        nc.vector.memset(bias_a[:].bitcast(I32), 0)
-        nc.vector.memset(x_scales[:].bitcast(I32), 0)
-        nc.vector.memset(w_scales[0][:].bitcast(I32), 0)
         nc.vector.memset(warm[:].bitcast(I32), 0)
-        nc.vector.memset(sel[:].bitcast(I32), 0)
-        for j in range(4):
-            nc.vector.memset(sel[32 * j : 32 * j + 1, j, :], 1.0)
+        for first_pass in (0, 2):
+            nc.vector.memset(x_scales[:, first_pass : first_pass + 2, :].bitcast(I32), 0)
+            nc.vector.memset(w_scales[0][:, first_pass : first_pass + 2, :].bitcast(I32), 0)
         nc.vector.memset(bias_rows[:].bitcast(I32), 0)
         nc.vector.memset(w_scales[1][:].bitcast(I32), 0)
+        nc.vector.memset(w_scales[2][:].bitcast(I32), 0)
 
-        make_identity(nc, ident[:])
         nc.gpsimd.dma_start(out=bias_rows[0:16, :], in_=bias_gate.rearrange("o (r c) -> (o r) c", c=256))
         nc.gpsimd.dma_start(out=bias_rows[16:32, :], in_=bias_update.rearrange("o (r c) -> (o r) c", c=256))
+        make_identity(nc, ident[:])
+        nc.gpsimd.dma_start(out=zeta_b[:], in_=zeta.rearrange("a b -> (a b)").partition_broadcast(P))
+        nc.gpsimd.dma_start(out=nu_b[:], in_=nu.rearrange("a b -> (a b)").partition_broadcast(P))
+        nc.vector.tensor_copy(out=ident_bf[:], in_=ident[:])
 
         def load_scales(plane, first_pass, src, lo, hi):
             for q in range(4):
@@ -134,22 +134,20 @@ def tile_fastgrnncudacell_pa_kernel(
 
         load_codes(x_codes, 0, wx_r_words, 0, B)
         load_codes(w_codes[0], 0, W2_words, *CHUNKS[0])
-        for i, bias in enumerate((bias_gate, bias_update)):
-            nc.sync.dma_start(out=bias_a[64 * i : 64 * (i + 1) : 32, :], in_=bias.rearrange("o (r c) -> (o r) c", c=A_HALF)[0:2, :])
         load_scales(x_scales, 0, wx_r_scales, 0, B)
         load_scales(w_scales[0], 0, W2_scales, *SCALE_CHUNKS[0])
         load_codes(x_codes, 2, uh_r_words, 0, B)
         load_codes(w_codes[0], 2, U2_words, *CHUNKS[0])
         load_scales(x_scales, 2, uh_r_scales, 0, B)
         load_scales(w_scales[0], 2, U2_scales, *SCALE_CHUNKS[0])
-        nc.sync.dma_start(out=zeta_b[:], in_=zeta.rearrange("a b -> (a b)").partition_broadcast(P))
-        nc.sync.dma_start(out=nu_b[:], in_=nu.rearrange("a b -> (a b)").partition_broadcast(P))
-        load_scales(w_scales[1], 0, W2_scales, *SCALE_CHUNKS[1])
-        load_scales(w_scales[1], 2, U2_scales, *SCALE_CHUNKS[1])
         load_codes(w_codes[1], 0, W2_words, *CHUNKS[1])
         load_codes(w_codes[1], 2, U2_words, *CHUNKS[1])
+        load_scales(w_scales[1], 0, W2_scales, *SCALE_CHUNKS[1])
+        load_scales(w_scales[1], 2, U2_scales, *SCALE_CHUNKS[1])
         load_state(0)
         load_state(1)
+        load_scales(w_scales[2], 0, W2_scales, *SCALE_CHUNKS[2])
+        load_scales(w_scales[2], 2, U2_scales, *SCALE_CHUNKS[2])
         for i in (2, 3):
             load_codes(w_codes[i], 0, W2_words, *CHUNKS[i])
             load_codes(w_codes[i], 2, U2_words, *CHUNKS[i])
@@ -200,9 +198,9 @@ def tile_fastgrnncudacell_pa_kernel(
         def store_a(p):
             nc.sync.dma_start(out=out[P * p : P * (p + 1), 0:A_CH], in_=s1[p][:])
 
-        def warm_up(n):
+        def warm_up():
             t, k = take_bank([P, B], "warm_ps")
-            for i in range(n):
+            for i in range(N_WARM):
                 nc.tensor.matmul(out=t[:], lhsT=warm[:, 0:P], rhs=warm[:], start=True, stop=True)
             give_bank(k)
 
@@ -210,16 +208,31 @@ def tile_fastgrnncudacell_pa_kernel(
             for i in range(2):
                 for half in range(A_CH // A_HALF):
                     t, k = take_bank([P, A_HALF], "bc_ps")
-                    nc.tensor.matmul(out=t[:], lhsT=sel[:, 2 * i + half, :], rhs=bias_a[:], start=True, stop=True)
+                    for e in range(2):
+                        r = 16 * i + 2 * half + e
+                        nc.tensor.matmul(
+                            out=t[:, 256 * e : 256 * (e + 1)],
+                            lhsT=ident_bf[:, r : r + 1].to_broadcast([P, P]),
+                            rhs=bias_rows[:],
+                            start=True,
+                            stop=True,
+                        )
                     nc.scalar.copy(out=bias_bc[i][:, A_HALF * half : A_HALF * (half + 1)], in_=t[:])
                     give_bank(k)
 
         def turn_biases():
+            nc.vector.tensor_copy(out=bias_sq[:], in_=bias_rows[:])
             t, k = take_bank([P, 2, P], "bias_ps")
             for e in range(2):
                 nc.tensor.transpose(t[:, e, :], bias_sq[:, P * e : P * (e + 1)], ident[:])
-            nc.scalar.copy(out=bias_t[:], in_=t[:, :, 0:32])
+            nc.vector.tensor_copy(out=bias_t[:], in_=t[:, :, 0:32])
             give_bank(k)
+
+        def make_consts():
+            nc.scalar.activation(out=consts[:, 0:1], in_=zeta_b[:], func=ACT.Sigmoid)
+            nc.scalar.activation(out=consts[:, 1:2], in_=nu_b[:], func=ACT.Sigmoid)
+            nc.vector.tensor_add(out=consts[:, 2:3], in0=consts[:, 0:1], in1=consts[:, 1:2])
+            nc.vector.tensor_scalar_mul(out=consts[:, 3:4], in0=consts[:, 0:1], scalar1=-1.0)
 
         steps = [[b, b + 1] for b in range(FIRST_B, N_BLOCKS - 2, 2)] + [[N_BLOCKS - 2], [N_BLOCKS - 1]]
 
@@ -317,26 +330,21 @@ def tile_fastgrnncudacell_pa_kernel(
                         give_bank(banks[(b, "c")][1])
 
         units = [(p, half) for p in range(TOK_TILES) for half in range(A_CH // A_HALF)]
-        warm_up(N_WARM[0])
-        spread_biases()
-        warm_up(N_WARM[1])
-        for p, half in units:
+        warm_up()
+        for p, half in units[0:4]:
             multiply_a(p, half, (0, 1))
-        nc.scalar.copy(out=bias_sq[:], in_=bias_rows[:])
-        nc.scalar.activation(out=consts[:, 0:1], in_=zeta_b[:], func=ACT.Sigmoid)
-        nc.scalar.activation(out=consts[:, 1:2], in_=nu_b[:], func=ACT.Sigmoid)
-        for i, (p, half) in enumerate(units):
+        spread_biases()
+        turn_biases()
+        make_consts()
+        for p, half in units[4:8]:
+            multiply_a(p, half, (0, 1))
+        for p, half in units:
             multiply_a(p, half, (2, 3))
             add_biases(p, half)
-            if i == 3:
-                nc.vector.tensor_add(out=consts[:, 2:3], in0=consts[:, 0:1], in1=consts[:, 1:2])
-                nc.vector.tensor_scalar_mul(out=consts[:, 3:4], in0=consts[:, 0:1], scalar1=-1.0)
-        gates_a(0)
-        turn_biases()
 
         for s in range(len(steps) + 1):
             for p in range(TOK_TILES):
-                if GATES_A_AT[p] == s and p > 0:
+                if GATES_A_AT[p] == s:
                     gates_a(p)
                 if STORE_A_AT[p] == s:
                     store_a(p)
@@ -350,6 +358,6 @@ def tile_fastgrnncudacell_pa_kernel(
                         candidate_weight(b)
             if s >= 1:
                 blocks = steps[s - 1]
-                o_tile = work.tile([P, TOK_TILES, len(blocks) * P], F32, name="o_tile", tag="o_tile")
+                o_tile = work.tile([P, TOK_TILES, len(blocks) * P], F32, name="o_tile", tag="o_tile", bufs=6)
                 finish(blocks, o_tile)
                 nc.sync.dma_start(out=out_v[:, :, P * blocks[0] : P * (blocks[-1] + 1)], in_=o_tile[:])

@@ -133,12 +133,12 @@ def tile_fastgrnncudacell_pa_kernel(
             nc.sync.dma_start(out=st[i][:], in_=state_v[:, :, CHUNKS[i][0] : CHUNKS[i][1]])
 
         load_codes(x_codes, 0, wx_r_words, 0, B)
-        load_codes(w_codes[0], 0, W2_words, *CHUNKS[0])
         load_scales(x_scales, 0, wx_r_scales, 0, B)
+        load_codes(w_codes[0], 0, W2_words, *CHUNKS[0])
         load_scales(w_scales[0], 0, W2_scales, *SCALE_CHUNKS[0])
         load_codes(x_codes, 2, uh_r_words, 0, B)
-        load_codes(w_codes[0], 2, U2_words, *CHUNKS[0])
         load_scales(x_scales, 2, uh_r_scales, 0, B)
+        load_codes(w_codes[0], 2, U2_words, *CHUNKS[0])
         load_scales(w_scales[0], 2, U2_scales, *SCALE_CHUNKS[0])
         load_codes(w_codes[1], 0, W2_words, *CHUNKS[1])
         load_codes(w_codes[1], 2, U2_words, *CHUNKS[1])

@@ -96,15 +96,21 @@ def tile_fastgrnncudacell_pa_kernel(
         nu_b = keep.tile([P, 1], BF16, name="nu_b")
         consts = keep.tile([P, 4], F32, name="consts")
         ident = keep.tile([P, P], F32, name="ident")
-        ident_bf = keep.tile([P, P], BF16, name="ident_bf")
+        bias4 = keep.tile([P, A_HALF], BF16, name="bias4")
+        onehot = keep.tile([P, 4, P], BF16, name="onehot")
         warm = keep.tile([P, B], BF16, name="warm")
         a_col = consts[:, 2:3]
         nsz_col = consts[:, 3:4]
 
         nc.vector.memset(warm[:].bitcast(I32), 0)
+        nc.vector.memset(bias4[:].bitcast(I32), 0)
         for first_pass in (0, 2):
             nc.vector.memset(x_scales[:, first_pass : first_pass + 2, :].bitcast(I32), 0)
             nc.vector.memset(w_scales[0][:, first_pass : first_pass + 2, :].bitcast(I32), 0)
+            if first_pass == 0:
+                nc.vector.memset(onehot[:].bitcast(I32), 0)
+                for k in range(4):
+                    nc.vector.memset(onehot[32 * k : 32 * k + 1, k, :], 1.0)
         nc.vector.memset(bias_rows[:].bitcast(I32), 0)
         nc.vector.memset(w_scales[1][:].bitcast(I32), 0)
         nc.vector.memset(w_scales[2][:].bitcast(I32), 0)
@@ -114,7 +120,6 @@ def tile_fastgrnncudacell_pa_kernel(
         make_identity(nc, ident[:])
         nc.gpsimd.dma_start(out=zeta_b[:], in_=zeta.rearrange("a b -> (a b)").partition_broadcast(P))
         nc.gpsimd.dma_start(out=nu_b[:], in_=nu.rearrange("a b -> (a b)").partition_broadcast(P))
-        nc.vector.tensor_copy(out=ident_bf[:], in_=ident[:])
 
         def load_scales(plane, first_pass, src, lo, hi):
             for q in range(4):
@@ -133,6 +138,8 @@ def tile_fastgrnncudacell_pa_kernel(
             nc.sync.dma_start(out=st[i][:], in_=state_v[:, :, CHUNKS[i][0] : CHUNKS[i][1]])
 
         load_codes(x_codes, 0, wx_r_words, 0, B)
+        nc.sync.dma_start(out=bias4[0:64:32, :], in_=bias_gate.rearrange("o (r c) -> (o r) c", c=A_HALF)[0:2, :])
+        nc.sync.dma_start(out=bias4[64:128:32, :], in_=bias_update.rearrange("o (r c) -> (o r) c", c=A_HALF)[0:2, :])
         load_scales(x_scales, 0, wx_r_scales, 0, B)
         load_codes(w_codes[0], 0, W2_words, *CHUNKS[0])
         load_scales(w_scales[0], 0, W2_scales, *SCALE_CHUNKS[0])
@@ -208,16 +215,11 @@ def tile_fastgrnncudacell_pa_kernel(
             for i in range(2):
                 for half in range(A_CH // A_HALF):
                     t, k = take_bank([P, A_HALF], "bc_ps")
-                    for e in range(2):
-                        r = 16 * i + 2 * half + e
-                        nc.tensor.matmul(
-                            out=t[:, 256 * e : 256 * (e + 1)],
-                            lhsT=ident_bf[:, r : r + 1].to_broadcast([P, P]),
-                            rhs=bias_rows[:],
-                            start=True,
-                            stop=True,
-                        )
-                    nc.scalar.copy(out=bias_bc[i][:, A_HALF * half : A_HALF * (half + 1)], in_=t[:])
+                    nc.tensor.matmul(out=t[:], lhsT=onehot[:, 2 * i + half, :], rhs=bias4[:], start=True, stop=True)
+                    if half == 0:
+                        nc.scalar.copy(out=bias_bc[i][:, A_HALF * half : A_HALF * (half + 1)], in_=t[:])
+                    else:
+                        nc.vector.tensor_copy(out=bias_bc[i][:, A_HALF * half : A_HALF * (half + 1)], in_=t[:])
                     give_bank(k)
 
         def turn_biases():
@@ -331,9 +333,9 @@ def tile_fastgrnncudacell_pa_kernel(
 
         units = [(p, half) for p in range(TOK_TILES) for half in range(A_CH // A_HALF)]
         warm_up()
+        spread_biases()
         for p, half in units[0:4]:
             multiply_a(p, half, (0, 1))
-        spread_biases()
         turn_biases()
         make_consts()
         for p, half in units[4:8]:

@@ -138,8 +138,8 @@ def tile_fastgrnncudacell_pa_kernel(
             nc.sync.dma_start(out=st[i][:], in_=state_v[:, :, CHUNKS[i][0] : CHUNKS[i][1]])
 
         load_codes(x_codes, 0, wx_r_words, 0, B)
-        nc.sync.dma_start(out=bias4[0:64:32, :], in_=bias_gate.rearrange("o (r c) -> (o r) c", c=A_HALF)[0:2, :])
-        nc.sync.dma_start(out=bias4[64:128:32, :], in_=bias_update.rearrange("o (r c) -> (o r) c", c=A_HALF)[0:2, :])
+        nc.scalar.dma_start(out=bias4[0:64:32, :], in_=bias_gate.rearrange("o (r c) -> (o r) c", c=A_HALF)[0:2, :])
+        nc.scalar.dma_start(out=bias4[64:128:32, :], in_=bias_update.rearrange("o (r c) -> (o r) c", c=A_HALF)[0:2, :])
         load_scales(x_scales, 0, wx_r_scales, 0, B)
         load_codes(w_codes[0], 0, W2_words, *CHUNKS[0])
         load_scales(w_scales[0], 0, W2_scales, *SCALE_CHUNKS[0])

@@ -267,8 +267,12 @@ def tile_fastgrnncudacell_pa_kernel(
             ct = work.tile([P, B], F32, name="c_t", tag="c_t", bufs=6)
             acc, k = pre[b]
             r, e = b // 2, b % 2
-            nc.scalar.activation(out=zt[:], in_=acc[:], func=ACT.Sigmoid, bias=bias_t[:, e, r : r + 1], scale=1.0)
-            nc.scalar.activation(out=ct[:], in_=acc[:], func=ACT.Tanh, bias=bias_t[:, e, 16 + r : 17 + r], scale=1.0)
+            if on_gpsimd(b):
+                nc.scalar.activation(out=zt[:], in_=acc[:], func=ACT.Sigmoid, bias=bias_t[:, e, r : r + 1], scale=1.0)
+                nc.scalar.activation(out=ct[:], in_=acc[:], func=ACT.Tanh, bias=bias_t[:, e, 16 + r : 17 + r], scale=1.0)
+            else:
+                nc.scalar.activation(out=ct[:], in_=acc[:], func=ACT.Tanh, bias=bias_t[:, e, 16 + r : 17 + r], scale=1.0)
+                nc.scalar.activation(out=zt[:], in_=acc[:], func=ACT.Sigmoid, bias=bias_t[:, e, r : r + 1], scale=1.0)
             give_bank(k)
             z_t[b] = zt
             c_t[b] = ct
@@ -362,4 +366,8 @@ def tile_fastgrnncudacell_pa_kernel(
                 blocks = steps[s - 1]
                 o_tile = work.tile([P, TOK_TILES, len(blocks) * P], F32, name="o_tile", tag="o_tile", bufs=6)
                 finish(blocks, o_tile)
-                nc.sync.dma_start(out=out_v[:, :, P * blocks[0] : P * (blocks[-1] + 1)], in_=o_tile[:])
+                if s == len(steps):
+                    for h in (slice(0, 2), slice(2, 4)):
+                        nc.sync.dma_start(out=out_v[:, h, P * blocks[0] : P * (blocks[-1] + 1)], in_=o_tile[:, h, :])
+                else:
+                    nc.sync.dma_start(out=out_v[:, :, P * blocks[0] : P * (blocks[-1] + 1)], in_=o_tile[:])

@@ -262,6 +262,53 @@ def tile_fastgrnncudacell_pa_kernel(
                     stop=(g == PASSES - 1),
                 )
 
+        def multiply_halves(b):
+            ci, coff = find_chunk(CHUNKS, P * b)
+            si, soff = find_chunk(SCALE_CHUNKS, P * b)
+            pre[b] = take_bank([P, B], "pre")
+            for h in range(2):
+                for g in range(PASSES):
+                    nc.tensor.matmul_mx(
+                        out=pre[b][0][:, (B // 2) * h : (B // 2) * (h + 1)],
+                        lhsT=w_codes[ci][:, g, 2 * coff : 2 * (coff + P)].bitcast(FP4X4),
+                        lhsT_scale=w_scales[si][:, g, soff : soff + P],
+                        rhs=x_codes[:, g, B * h : B * (h + 1)].bitcast(FP4X4),
+                        rhs_scale=x_scales[:, g, (B // 2) * h : (B // 2) * (h + 1)],
+                        start=(g == 0),
+                        stop=(g == PASSES - 1),
+                    )
+
+        def activate_halves(b):
+            zt = work.tile([P, B], F32, name="z_t", tag="z_t", bufs=6)
+            ct = work.tile([P, B], F32, name="c_t", tag="c_t", bufs=6)
+            acc, k = pre[b]
+            r, e = b // 2, b % 2
+            for h in range(2):
+                cols = slice((B // 2) * h, (B // 2) * (h + 1))
+                nc.scalar.activation(out=ct[:, cols], in_=acc[:, cols], func=ACT.Tanh, bias=bias_t[:, e, 16 + r : 17 + r], scale=1.0)
+                nc.scalar.activation(out=zt[:, cols], in_=acc[:, cols], func=ACT.Sigmoid, bias=bias_t[:, e, r : r + 1], scale=1.0)
+            give_bank(k)
+            z_t[b] = zt
+            c_t[b] = ct
+
+        def finish_halves(b, o_tile):
+            t1 = work.tile([P, TOK_TILES, P], F32, name="t1", tag="t1")
+            t2 = work.tile([P, TOK_TILES, P], F32, name="t2", tag="t2")
+            c_bank, c_k = take_bank([P, TOK_TILES, P], "tr")
+            z_bank, z_k = take_bank([P, TOK_TILES, P], "tr")
+            for h in (slice(0, 2), slice(2, 4)):
+                for bank, src in ((c_bank, c_t[b]), (z_bank, z_t[b])):
+                    for t in range(h.start, h.stop):
+                        nc.tensor.transpose(bank[:, t, :], src[:, P * t : P * (t + 1)], ident[:])
+            for h in (slice(0, 2), slice(2, 4)):
+                nc.vector.scalar_tensor_tensor(out=t1[:, h, :], in0=c_bank[:, h, :], scalar=nsz_col, in1=state_view(b)[:, h, :], op0=ALU.mult, op1=ALU.add)
+            for h in (slice(0, 2), slice(2, 4)):
+                nc.vector.tensor_tensor(out=t2[:, h, :], in0=t1[:, h, :], in1=z_bank[:, h, :], op=ALU.mult)
+            for h in (slice(0, 2), slice(2, 4)):
+                nc.vector.scalar_tensor_tensor(out=o_tile[:, h, :], in0=c_bank[:, h, :], scalar=a_col, in1=t2[:, h, :], op0=ALU.mult, op1=ALU.add)
+            give_bank(z_k)
+            give_bank(c_k)
+
         def activate(b):
             zt = work.tile([P, B], F32, name="z_t", tag="z_t", bufs=6)
             ct = work.tile([P, B], F32, name="c_t", tag="c_t", bufs=6)
@@ -355,17 +402,24 @@ def tile_fastgrnncudacell_pa_kernel(
                 if STORE_A_AT[p] == s:
                     store_a(p)
             if s < len(steps):
-                for b in steps[s]:
-                    multiply(b)
-                for b in steps[s]:
-                    activate(b)
+                if s == len(steps) - 1:
+                    multiply_halves(steps[s][0])
+                    activate_halves(steps[s][0])
+                else:
+                    for b in steps[s]:
+                        multiply(b)
+                    for b in steps[s]:
+                        activate(b)
                 for b in steps[s]:
                     if on_gpsimd(b):
                         candidate_weight(b)
             if s >= 1:
                 blocks = steps[s - 1]
                 o_tile = work.tile([P, TOK_TILES, len(blocks) * P], F32, name="o_tile", tag="o_tile", bufs=6)
-                finish(blocks, o_tile)
+                if s == len(steps):
+                    finish_halves(blocks[0], o_tile)
+                else:
+                    finish(blocks, o_tile)
                 if s == len(steps):
                     for h in (slice(0, 2), slice(2, 4)):
                         nc.sync.dma_start(out=out_v[:, h, P * blocks[0] : P * (blocks[-1] + 1)], in_=o_tile[:, h, :])

from contextlib import ExitStack

import concourse.mybir as mybir
from concourse.masks import make_identity

B, D_H, RANK = 512, 4096, 1024
FLOPS = 2 * B * D_H * 2 * RANK

F32 = mybir.dt.float32
BF16 = mybir.dt.bfloat16
U8 = mybir.dt.uint8
I32 = mybir.dt.int32
FP4X4 = mybir.dt.float4_e2m1fn_x4
ACT = mybir.ActivationFunctionType
ALU = mybir.AluOpType

P = 128
PASSES = 4
TOK_TILES = B // P
N_BLOCKS = D_H // P
N_BANKS = 8
N_WARM = 8

A_CH = 1024
A_HALF = 512
FIRST_B = A_CH // P

CHUNKS = ((0, 1024), (1024, 2048), (2048, 3072), (3072, 4096))
SCALE_CHUNKS = ((0, 1024), (1024, 2048), (2048, 4096))

GPSIMD_BLOCKS = (26, 28, 30)
GATES_A_AT = (0, 2, 4, 7)
STORE_A_AT = (2, 5, 7, 10)


def find_chunk(chunks, channel):
    for i, (lo, hi) in enumerate(chunks):
        if lo <= channel < hi:
            return i, channel - lo
    raise ValueError("channel outside every chunk")


def tile_fastgrnncudacell_pa_kernel(
    tc,
    wx_r_words,
    wx_r_scales,
    uh_r_words,
    uh_r_scales,
    state,
    W2_words,
    W2_scales,
    U2_words,
    U2_scales,
    bias_gate,
    bias_update,
    zeta,
    nu,
    out,
):
    nc = tc.nc
    state_v = state.rearrange("(t p) c -> p t c", p=P)
    out_v = out.rearrange("(t p) c -> p t c", p=P)

    with ExitStack() as ctx:
        keep = ctx.enter_context(tc.tile_pool(name="keep", bufs=1))
        work = ctx.enter_context(tc.tile_pool(name="work", bufs=4))
        psum = ctx.enter_context(tc.psum_pool(name="psum", bufs=1))
        ctx.enter_context(tc.manual_schedule())

        free_banks = list(range(N_BANKS))

        def take_bank(shape, name):
            k = free_banks.pop(0)
            t = psum.tile(shape, F32, name=name, tag="bank%d" % k)
            return t, k

        def give_bank(k):
            free_banks.append(k)

        x_codes = keep.tile([P, PASSES, 2 * B], U8, name="x_codes", align_bytes=64)
        x_scales = keep.tile([P, PASSES, B], U8, name="x_scales", align_bytes=64)
        w_codes = []
        st = []
        for i, (lo, hi) in enumerate(CHUNKS):
            w_codes.append(keep.tile([P, PASSES, 2 * (hi - lo)], U8, name="w_codes%d" % i, align_bytes=64))
            st.append(keep.tile([P, TOK_TILES, hi - lo], BF16, name="st%d" % i))
        w_scales = []
        for i, (lo, hi) in enumerate(SCALE_CHUNKS):
            w_scales.append(keep.tile([P, PASSES, hi - lo], U8, name="w_scales%d" % i, align_bytes=64))

        bias_rows = keep.tile([P, 256], BF16, name="bias_rows")
        bias_sq = keep.tile([P, 256], F32, name="bias_sq")
        bias_t = keep.tile([P, 2, 32], F32, name="bias_t")
        bias_bc = [keep.tile([P, A_CH], F32, name="bias_bc%d" % i) for i in range(2)]
        zeta_b = keep.tile([P, 1], BF16, name="zeta_b")
        nu_b = keep.tile([P, 1], BF16, name="nu_b")
        consts = keep.tile([P, 4], F32, name="consts")
        ident = keep.tile([P, P], F32, name="ident")
        bias4 = keep.tile([P, A_HALF], BF16, name="bias4")
        onehot = keep.tile([P, 4, P], BF16, name="onehot")
        warm = keep.tile([P, B], BF16, name="warm")
        a_col = consts[:, 2:3]
        nsz_col = consts[:, 3:4]

        nc.vector.memset(warm[:].bitcast(I32), 0)
        nc.vector.memset(bias4[:].bitcast(I32), 0)
        for first_pass in (0, 2):
            nc.vector.memset(x_scales[:, first_pass : first_pass + 2, :].bitcast(I32), 0)
            nc.vector.memset(w_scales[0][:, first_pass : first_pass + 2, :].bitcast(I32), 0)
            if first_pass == 0:
                nc.vector.memset(onehot[:].bitcast(I32), 0)
                for k in range(4):
                    nc.vector.memset(onehot[32 * k : 32 * k + 1, k, :], 1.0)
        nc.vector.memset(bias_rows[:].bitcast(I32), 0)
        nc.vector.memset(w_scales[1][:].bitcast(I32), 0)
        nc.vector.memset(w_scales[2][:].bitcast(I32), 0)

        nc.gpsimd.dma_start(out=bias_rows[0:16, :], in_=bias_gate.rearrange("o (r c) -> (o r) c", c=256))
        nc.gpsimd.dma_start(out=bias_rows[16:32, :], in_=bias_update.rearrange("o (r c) -> (o r) c", c=256))
        make_identity(nc, ident[:])
        nc.gpsimd.dma_start(out=zeta_b[:], in_=zeta.rearrange("a b -> (a b)").partition_broadcast(P))
        nc.gpsimd.dma_start(out=nu_b[:], in_=nu.rearrange("a b -> (a b)").partition_broadcast(P))

        def load_scales(plane, first_pass, src, lo, hi):
            for q in range(4):
                nc.sync.dma_start(
                    out=plane[32 * q : 32 * q + 4, first_pass : first_pass + 2, :].bitcast(I32),
                    in_=src[:, 4 * q : 4 * q + 4, lo:hi].rearrange("g r n -> r g n").bitcast(I32),
                )

        def load_codes(tile, first_pass, src, lo, hi):
            nc.sync.dma_start(
                out=tile[:, first_pass : first_pass + 2, :].bitcast(I32),
                in_=src[:, :, 2 * lo : 2 * hi].rearrange("g p n -> p g n").bitcast(I32),
            )

        def load_state(i):
            nc.sync.dma_start(out=st[i][:], in_=state_v[:, :, CHUNKS[i][0] : CHUNKS[i][1]])

        load_codes(x_codes, 0, wx_r_words, 0, B)
        nc.scalar.dma_start(out=bias4[0:64:32, :], in_=bias_gate.rearrange("o (r c) -> (o r) c", c=A_HALF)[0:2, :])
        nc.scalar.dma_start(out=bias4[64:128:32, :], in_=bias_update.rearrange("o (r c) -> (o r) c", c=A_HALF)[0:2, :])
        load_scales(x_scales, 0, wx_r_scales, 0, B)
        load_codes(w_codes[0], 0, W2_words, *CHUNKS[0])
        load_scales(w_scales[0], 0, W2_scales, *SCALE_CHUNKS[0])
        load_codes(x_codes, 2, uh_r_words, 0, B)
        load_scales(x_scales, 2, uh_r_scales, 0, B)
        load_codes(w_codes[0], 2, U2_words, *CHUNKS[0])
        load_scales(w_scales[0], 2, U2_scales, *SCALE_CHUNKS[0])
        load_codes(w_codes[1], 0, W2_words, *CHUNKS[1])
        load_codes(w_codes[1], 2, U2_words, *CHUNKS[1])
        load_scales(w_scales[1], 0, W2_scales, *SCALE_CHUNKS[1])
        load_scales(w_scales[1], 2, U2_scales, *SCALE_CHUNKS[1])
        load_state(0)
        load_state(1)
        load_scales(w_scales[2], 0, W2_scales, *SCALE_CHUNKS[2])
        load_scales(w_scales[2], 2, U2_scales, *SCALE_CHUNKS[2])
        for i in (2, 3):
            load_codes(w_codes[i], 0, W2_words, *CHUNKS[i])
            load_codes(w_codes[i], 2, U2_words, *CHUNKS[i])
            load_state(i)

        acc_a = {}
        s1 = {}
        s2 = {}
        g_a = {}

        def multiply_a(p, half, passes):
            if (p, half) not in acc_a:
                acc_a[(p, half)] = take_bank([P, A_HALF], "acc_a")
            acc = acc_a[(p, half)][0]
            for g in passes:
                nc.tensor.matmul_mx(
                    out=acc[:],
                    lhsT=x_codes[:, g, 2 * P * p : 2 * P * (p + 1)].bitcast(FP4X4),
                    lhsT_scale=x_scales[:, g, P * p : P * (p + 1)],
                    rhs=w_codes[0][:, g, 2 * A_HALF * half : 2 * A_HALF * (half + 1)].bitcast(FP4X4),
                    rhs_scale=w_scales[0][:, g, A_HALF * half : A_HALF * (half + 1)],
                    start=(g == 0),
                    stop=(g == PASSES - 1),
                )

        def add_biases(p, half):
            if p not in s1:
                s1_tile = work.tile([P, A_CH], F32, name="s1", tag="s1")
                s2_tile = work.tile([P, A_CH], F32, name="s2", tag="s2")
                s1[p] = s1_tile
                s2[p] = s2_tile
            acc, k = acc_a[(p, half)]
            cols = slice(A_HALF * half, A_HALF * (half + 1))
            nc.vector.tensor_tensor(out=s1[p][:, cols], in0=acc[:], in1=bias_bc[0][:, cols], op=ALU.add)
            nc.vector.tensor_tensor(out=s2[p][:, cols], in0=acc[:], in1=bias_bc[1][:, cols], op=ALU.add)
            give_bank(k)

        def gates_a(p):
            g_tile = work.tile([P, A_CH], F32, name="g_a", tag="g_a")
            g_a[p] = g_tile
            nc.scalar.activation(out=s1[p][:], in_=s1[p][:], func=ACT.Sigmoid)
            nc.scalar.activation(out=s2[p][:], in_=s2[p][:], func=ACT.Tanh)
            nc.scalar.activation(out=g_tile[:], in_=s1[p][:], func=ACT.Identity, bias=a_col, scale=nsz_col)
            nc.gpsimd.tensor_tensor(out=g_tile[:], in0=g_tile[:], in1=s2[p][:], op=ALU.mult)
            nc.gpsimd.tensor_tensor(out=s1[p][:], in0=s1[p][:], in1=st[0][:, p, :], op=ALU.mult)
            nc.gpsimd.tensor_tensor(out=s1[p][:], in0=s1[p][:], in1=g_tile[:], op=ALU.add)

        def store_a(p):
            nc.sync.dma_start(out=out[P * p : P * (p + 1), 0:A_CH], in_=s1[p][:])

        def warm_up():
            t, k = take_bank([P, B], "warm_ps")
            for i in range(N_WARM):
                nc.tensor.matmul(out=t[:], lhsT=warm[:, 0:P], rhs=warm[:], start=True, stop=True)
            give_bank(k)

        def spread_biases():
            for i in range(2):
                for half in range(A_CH // A_HALF):
                    t, k = take_bank([P, A_HALF], "bc_ps")
                    nc.tensor.matmul(out=t[:], lhsT=onehot[:, 2 * i + half, :], rhs=bias4[:], start=True, stop=True)
                    if half == 0:
                        nc.scalar.copy(out=bias_bc[i][:, A_HALF * half : A_HALF * (half + 1)], in_=t[:])
                    else:
                        nc.vector.tensor_copy(out=bias_bc[i][:, A_HALF * half : A_HALF * (half + 1)], in_=t[:])
                    give_bank(k)

        def turn_biases():
            nc.vector.tensor_copy(out=bias_sq[:], in_=bias_rows[:])
            t, k = take_bank([P, 2, P], "bias_ps")
            for e in range(2):
                nc.tensor.transpose(t[:, e, :], bias_sq[:, P * e : P * (e + 1)], ident[:])
            nc.vector.tensor_copy(out=bias_t[:], in_=t[:, :, 0:32])
            give_bank(k)

        def make_consts():
            nc.scalar.activation(out=consts[:, 0:1], in_=zeta_b[:], func=ACT.Sigmoid)
            nc.scalar.activation(out=consts[:, 1:2], in_=nu_b[:], func=ACT.Sigmoid)
            nc.vector.tensor_add(out=consts[:, 2:3], in0=consts[:, 0:1], in1=consts[:, 1:2])
            nc.vector.tensor_scalar_mul(out=consts[:, 3:4], in0=consts[:, 0:1], scalar1=-1.0)

        steps = [[b, b + 1] for b in range(FIRST_B, N_BLOCKS - 2, 2)] + [[N_BLOCKS - 2], [N_BLOCKS - 1]]

        def on_gpsimd(b):
            return b in GPSIMD_BLOCKS

        pre = {}
        z_t = {}
        c_t = {}
        h_t = {}
        banks = {}

        def multiply(b):
            ci, coff = find_chunk(CHUNKS, P * b)
            si, soff = find_chunk(SCALE_CHUNKS, P * b)
            pre[b] = take_bank([P, B], "pre")
            for g in range(PASSES):
                nc.tensor.matmul_mx(
                    out=pre[b][0][:],
                    lhsT=w_codes[ci][:, g, 2 * coff : 2 * (coff + P)].bitcast(FP4X4),
                    lhsT_scale=w_scales[si][:, g, soff : soff + P],
                    rhs=x_codes[:, g, :].bitcast(FP4X4),
                    rhs_scale=x_scales[:, g, :],
                    start=(g == 0),
                    stop=(g == PASSES - 1),
                )

        def multiply_halves(b):
            ci, coff = find_chunk(CHUNKS, P * b)
            si, soff = find_chunk(SCALE_CHUNKS, P * b)
            pre[b] = take_bank([P, B], "pre")
            for h in range(2):
                for g in range(PASSES):
                    nc.tensor.matmul_mx(
                        out=pre[b][0][:, (B // 2) * h : (B // 2) * (h + 1)],
                        lhsT=w_codes[ci][:, g, 2 * coff : 2 * (coff + P)].bitcast(FP4X4),
                        lhsT_scale=w_scales[si][:, g, soff : soff + P],
                        rhs=x_codes[:, g, B * h : B * (h + 1)].bitcast(FP4X4),
                        rhs_scale=x_scales[:, g, (B // 2) * h : (B // 2) * (h + 1)],
                        start=(g == 0),
                        stop=(g == PASSES - 1),
                    )

        def activate_halves(b):
            zt = work.tile([P, B], F32, name="z_t", tag="z_t", bufs=6)
            ct = work.tile([P, B], F32, name="c_t", tag="c_t", bufs=6)
            acc, k = pre[b]
            r, e = b // 2, b % 2
            for h in range(2):
                cols = slice((B // 2) * h, (B // 2) * (h + 1))
                nc.scalar.activation(out=ct[:, cols], in_=acc[:, cols], func=ACT.Tanh, bias=bias_t[:, e, 16 + r : 17 + r], scale=1.0)
                nc.scalar.activation(out=zt[:, cols], in_=acc[:, cols], func=ACT.Sigmoid, bias=bias_t[:, e, r : r + 1], scale=1.0)
            give_bank(k)
            z_t[b] = zt
            c_t[b] = ct

        def finish_halves(b, o_tile):
            t1 = work.tile([P, TOK_TILES, P], F32, name="t1", tag="t1")
            t2 = work.tile([P, TOK_TILES, P], F32, name="t2", tag="t2")
            c_bank, c_k = take_bank([P, TOK_TILES, P], "tr")
            z_bank, z_k = take_bank([P, TOK_TILES, P], "tr")
            for h in (slice(0, 2), slice(2, 4)):
                for bank, src in ((c_bank, c_t[b]), (z_bank, z_t[b])):
                    for t in range(h.start, h.stop):
                        nc.tensor.transpose(bank[:, t, :], src[:, P * t : P * (t + 1)], ident[:])
            for h in (slice(0, 2), slice(2, 4)):
                nc.vector.scalar_tensor_tensor(out=t1[:, h, :], in0=c_bank[:, h, :], scalar=nsz_col, in1=state_view(b)[:, h, :], op0=ALU.mult, op1=ALU.add)
            for h in (slice(0, 2), slice(2, 4)):
                nc.vector.tensor_tensor(out=t2[:, h, :], in0=t1[:, h, :], in1=z_bank[:, h, :], op=ALU.mult)
            for h in (slice(0, 2), slice(2, 4)):
                nc.vector.scalar_tensor_tensor(out=o_tile[:, h, :], in0=c_bank[:, h, :], scalar=a_col, in1=t2[:, h, :], op0=ALU.mult, op1=ALU.add)
            give_bank(z_k)
            give_bank(c_k)

        def activate(b):
            zt = work.tile([P, B], F32, name="z_t", tag="z_t", bufs=6)
            ct = work.tile([P, B], F32, name="c_t", tag="c_t", bufs=6)
            acc, k = pre[b]
            r, e = b // 2, b % 2
            if on_gpsimd(b):
                nc.scalar.activation(out=zt[:], in_=acc[:], func=ACT.Sigmoid, bias=bias_t[:, e, r : r + 1], scale=1.0)
                nc.scalar.activation(out=ct[:], in_=acc[:], func=ACT.Tanh, bias=bias_t[:, e, 16 + r : 17 + r], scale=1.0)
            else:
                nc.scalar.activation(out=ct[:], in_=acc[:], func=ACT.Tanh, bias=bias_t[:, e, 16 + r : 17 + r], scale=1.0)
                nc.scalar.activation(out=zt[:], in_=acc[:], func=ACT.Sigmoid, bias=bias_t[:, e, r : r + 1], scale=1.0)
            give_bank(k)
            z_t[b] = zt
            c_t[b] = ct

        def candidate_weight(b):
            gt = work.tile([P, B], F32, name="g_t", tag="g_t", bufs=2)
            ht = work.tile([P, B], F32, name="h_t", tag="h_t", bufs=2)
            nc.gpsimd.tensor_scalar(out=gt[:], in0=z_t[b][:], scalar1=nsz_col, scalar2=a_col, op0=ALU.mult, op1=ALU.add)
            nc.gpsimd.tensor_tensor(out=ht[:], in0=gt[:], in1=c_t[b][:], op=ALU.mult)
            h_t[b] = ht

        def turn(key, src):
            bank, k = take_bank([P, TOK_TILES, P], "tr")
            for t in range(TOK_TILES):
                nc.tensor.transpose(bank[:, t, :], src[:, P * t : P * (t + 1)], ident[:])
            banks[key] = (bank, k)

        def state_view(b):
            ci, coff = find_chunk(CHUNKS, P * b)
            return st[ci][:, :, coff : coff + P]

        def finish(blocks, o_tile):
            turns = []
            ops = []
            halves = (slice(0, 4),) if len(blocks) == 2 else (slice(0, 2), slice(2, 4))
            for i, b in enumerate(blocks):
                o_view = o_tile[:, :, P * i : P * (i + 1)]
                t1 = work.tile([P, TOK_TILES, P], F32, name="t1", tag="t1")
                if on_gpsimd(b):
                    turns.append([(z_t[b], (b, "z")), (h_t[b], (b, "h"))])
                    ops.append([("zs", b, t1, o_view), ("oh", b, t1, o_view)])
                else:
                    t2 = work.tile([P, TOK_TILES, P], F32, name="t2", tag="t2")
                    turns.append([(c_t[b], (b, "c")), (z_t[b], (b, "z"))])
                    ops.append([("u", b, t1, t2), ("v", b, t1, t2), ("oc", b, t2, o_view)])
            order = sorted(range(len(blocks)), key=lambda i: -len(ops[i]))
            for level in range(2):
                for i in order:
                    turn(turns[i][level][1], turns[i][level][0])
            for level in range(3):
                for i in order:
                    if level >= len(ops[i]):
                        continue
                    kind, b, x, y = ops[i][level]
                    for h in halves:
                        if kind == "zs":
                            nc.vector.tensor_tensor(out=x[:, h, :], in0=banks[(b, "z")][0][:, h, :], in1=state_view(b)[:, h, :], op=ALU.mult)
                        elif kind == "oh":
                            nc.vector.tensor_tensor(out=y[:, h, :], in0=banks[(b, "h")][0][:, h, :], in1=x[:, h, :], op=ALU.add)
                        elif kind == "u":
                            nc.vector.scalar_tensor_tensor(out=x[:, h, :], in0=banks[(b, "c")][0][:, h, :], scalar=nsz_col, in1=state_view(b)[:, h, :], op0=ALU.mult, op1=ALU.add)
                        elif kind == "v":
                            nc.vector.tensor_tensor(out=y[:, h, :], in0=x[:, h, :], in1=banks[(b, "z")][0][:, h, :], op=ALU.mult)
                        else:
                            nc.vector.scalar_tensor_tensor(out=y[:, h, :], in0=banks[(b, "c")][0][:, h, :], scalar=a_col, in1=x[:, h, :], op0=ALU.mult, op1=ALU.add)
                    if kind == "zs" or kind == "v":
                        give_bank(banks[(b, "z")][1])
                    elif kind == "oh":
                        give_bank(banks[(b, "h")][1])
                    elif kind == "oc":
                        give_bank(banks[(b, "c")][1])

        units = [(p, half) for p in range(TOK_TILES) for half in range(A_CH // A_HALF)]
        warm_up()
        spread_biases()
        for p, half in units[0:4]:
            multiply_a(p, half, (0, 1))
        turn_biases()
        make_consts()
        for p, half in units[4:8]:
            multiply_a(p, half, (0, 1))
        for p, half in units:
            multiply_a(p, half, (2, 3))
            add_biases(p, half)

        for s in range(len(steps) + 1):
            for p in range(TOK_TILES):
                if GATES_A_AT[p] == s:
                    gates_a(p)
                if STORE_A_AT[p] == s:
                    store_a(p)
            if s < len(steps):
                if s == len(steps) - 1:
                    multiply_halves(steps[s][0])
                    activate_halves(steps[s][0])
                else:
                    for b in steps[s]:
                        multiply(b)
                    for b in steps[s]:
                        activate(b)
                for b in steps[s]:
                    if on_gpsimd(b):
                        candidate_weight(b)
            if s >= 1:
                blocks = steps[s - 1]
                o_tile = work.tile([P, TOK_TILES, len(blocks) * P], F32, name="o_tile", tag="o_tile", bufs=6)
                if s == len(steps):
                    finish_halves(blocks[0], o_tile)
                else:
                    finish(blocks, o_tile)
                if s == len(steps):
                    for h in (slice(0, 2), slice(2, 4)):
                        nc.sync.dma_start(out=out_v[:, h, P * blocks[0] : P * (blocks[-1] + 1)], in_=o_tile[:, h, :])
                else:
                    nc.sync.dma_start(out=out_v[:, :, P * blocks[0] : P * (blocks[-1] + 1)], in_=o_tile[:])
